import numpy as np
import ml_dtypes


def mxq(x, axis, fmt="e4m3"):
    dtype, down = {"e4m3": (ml_dtypes.float8_e4m3fn, 7), "e5m2": (ml_dtypes.float8_e5m2, 14)}[fmt]
    v = np.moveaxis(np.asarray(x, np.float32).astype(ml_dtypes.bfloat16).astype(np.float64), axis, -1)
    blocks = v.reshape(v.shape[:-1] + (-1, 32))
    amax = np.abs(blocks).max(-1, keepdims=True)
    byte = np.maximum(np.where(amax > 0, np.frexp(amax)[1] - 1 + 127, 0) - down, 1)
    scale = np.exp2(byte - 127.0)
    codes = (blocks / scale).astype(np.float32).astype(dtype).astype(np.float64)
    return np.moveaxis((codes * scale).reshape(v.shape), -1, axis)


WIDE = False


def mx_kscale(k):
    if not WIDE:
        return np.ones(k)
    levels = np.array([10, -10, 5, -5, 0])
    a = np.random.permutation(np.resize(levels, k // 512 * 4)).reshape(k // 512, 4)
    idx = np.arange(k)
    return np.exp2(a[idx // 512, idx % 128 // 32])


BF16 = ml_dtypes.bfloat16


def bf(x):
    return np.asarray(x, np.float32).astype(BF16)


def f64(x):
    return np.asarray(x).astype(np.float64)


E2M1 = np.array([0.0, 0.5, 1.0, 1.5, 2.0, 3.0, 4.0, 6.0, -0.0, -0.5, -1.0, -1.5, -2.0, -3.0, -4.0, -6.0])


def pack_weight(w, fmt):
    k, n = w.shape
    w = f64(bf(w)).reshape(k // 32, 32, n)
    amax = np.abs(w).max(1)
    if fmt == "e4m3":
        byte = np.frexp(amax)[1] - 1 + 127 - 7
    else:
        mant, ex = np.frexp(amax / 6.0)
        byte = np.where(mant > 0.5, ex, ex - 1) + 127
    byte = np.clip(np.where(amax > 0, byte, 1), 1, 254)
    scaled = (w * np.exp2(127.0 - byte)[:, None, :]).reshape(k, n).astype(np.float32)
    by_word = np.ascontiguousarray(scaled.reshape(k // 512, 128, 4, n).transpose(0, 1, 3, 2))
    if fmt == "e4m3":
        words = by_word.astype(ml_dtypes.float8_e4m3fn).view(np.uint8)
    else:
        c = by_word.astype(ml_dtypes.float4_e2m1fn).view(np.uint8) & 0xF
        words = c[..., 0::2] | (c[..., 1::2] << 4)
    return np.ascontiguousarray(words), np.ascontiguousarray(byte.astype(np.uint8).reshape(k // 512, 16, n))


def unpack_weight(words, scales, fmt):
    g, p, n, _ = words.shape
    if fmt == "e4m3":
        vals = np.ascontiguousarray(words).view(ml_dtypes.float8_e4m3fn).astype(np.float64)
    else:
        nib = np.empty((g, p, n, 4), np.uint8)
        nib[..., 0::2] = words & 0xF
        nib[..., 1::2] = words >> 4
        vals = E2M1[nib]
    vals = vals * np.repeat(np.exp2(scales.astype(np.float64) - 127.0), 8, axis=1)[..., None]
    return vals.transpose(0, 1, 3, 2).reshape(g * 512, n)


B, SI, ST, DM, H, D = 1, 768, 256, 1024, 8, 128
S = ST + SI
HD = H * D
EPS = 1e-6
FMT = "e4m3"


def rms_norm(x, gamma):
    var = np.mean(x * x, axis=-1, keepdims=True)
    return x * (1.0 / np.sqrt(var + EPS)) * gamma


def apply_rotary(x, cos, sin):
    xr = x.reshape(B, S, H, D // 2, 2)
    x1, x2 = xr[..., 0], xr[..., 1]
    rot = np.stack([-x2, x1], axis=-1).reshape(B, S, H, D)
    return x * cos[None, :, None, :] + rot * sin[None, :, None, :]


def heads(y):
    return y.reshape(B, -1, H, D)


def setup_inputs():
    s = mx_kscale(DM)
    w = 1.0 / np.sqrt(DM)
    pos = np.arange(S)[:, None]
    inv = 1.0 / (10000.0 ** (np.arange(0, D, 2) / D))
    ang = np.repeat(pos * inv[None, :], 2, axis=-1)
    inp = {"hidden_states": bf(np.random.standard_normal((B, SI, DM)) * s),
           "encoder_hidden_states": bf(np.random.standard_normal((B, ST, DM)) * s),
           "rope_cos": bf(np.cos(ang)), "rope_sin": bf(np.sin(ang))}
    for n in ["Wq", "Wk", "Waq", "Wak"]:
        words, scales = pack_weight(np.random.standard_normal((DM, HD)) * w / s[:, None], FMT)
        inp[n + "_words"] = words
        inp[n + "_scales"] = scales
    for n in ["bq", "bk", "baq", "bak"]:
        inp[n] = bf(np.random.standard_normal(HD) * 0.3)
    for n in ["g_q", "g_k", "g_aq", "g_ak"]:
        inp[n] = bf(1.5 * (1.0 + 0.1 * np.random.standard_normal(D)))
    return inp


def reference(hidden_states, encoder_hidden_states, rope_cos, rope_sin, Wq_words, Wq_scales, bq, Wk_words, Wk_scales, bk, Waq_words, Waq_scales, baq, Wak_words, Wak_scales, bak, g_q, g_k, g_aq, g_ak):
    xq = mxq(f64(hidden_states), 2, "e4m3")
    cq = mxq(f64(encoder_hidden_states), 2, "e4m3")
    q = rms_norm(heads((xq @ unpack_weight(Wq_words, Wq_scales, FMT)) + f64(bq)), f64(g_q))
    k = rms_norm(heads((xq @ unpack_weight(Wk_words, Wk_scales, FMT)) + f64(bk)), f64(g_k))
    eq = rms_norm(heads((cq @ unpack_weight(Waq_words, Waq_scales, FMT)) + f64(baq)), f64(g_aq))
    ek = rms_norm(heads((cq @ unpack_weight(Wak_words, Wak_scales, FMT)) + f64(bak)), f64(g_ak))
    q = np.concatenate([eq, q], axis=1)
    k = np.concatenate([ek, k], axis=1)
    return apply_rotary(q, f64(rope_cos), f64(rope_sin)), apply_rotary(k, f64(rope_cos), f64(rope_sin))

@@ -1,0 +1,284 @@
+from contextlib import ExitStack
+
+import concourse.mybir as mybir
+from concourse.masks import make_identity
+
+F32 = mybir.dt.float32
+BF16 = mybir.dt.bfloat16
+I32 = mybir.dt.int32
+U32 = mybir.dt.uint32
+U8 = mybir.dt.uint8
+FP8X4 = mybir.dt.float8_e4m3fn_x4
+ACT = mybir.ActivationFunctionType
+ALU = mybir.AluOpType
+
+P = 128
+PACK = 4
+K_PASS = P * PACK
+MODEL = 1024
+PASSES = MODEL // K_PASS
+HEAD = 128
+HEADS = MODEL // HEAD
+PAIRS = HEAD // 2
+EPS = 1e-6
+
+TEXT_ROWS = 256
+SEQ = 1024
+GROUP_ROWS = 256
+GROUPS = SEQ // GROUP_ROWS
+GROUP_TILES = GROUP_ROWS // P
+ROW_TILES = SEQ // P
+STEP_HEADS = 4
+BANK_HEADS = 2
+
+FLOPS = 2 * SEQ * MODEL * 2 * MODEL
+
+
+def tile_fluxjointattention_pa_kernel(
+    tc,
+    hidden_states,
+    encoder_hidden_states,
+    rope_cos,
+    rope_sin,
+    Wq_words,
+    Wq_scales,
+    Wk_words,
+    Wk_scales,
+    Waq_words,
+    Waq_scales,
+    Wak_words,
+    Wak_scales,
+    bq,
+    bk,
+    baq,
+    bak,
+    g_q,
+    g_k,
+    g_aq,
+    g_ak,
+    out_0,
+    out_1,
+):
+    nc = tc.nc
+
+    words_in = [[Waq_words, Wak_words], [Wq_words, Wk_words]]
+    scales_in = [[Waq_scales, Wak_scales], [Wq_scales, Wk_scales]]
+    bias_in = [[baq, bak], [bq, bk]]
+    gain_in = [[g_aq, g_ak], [g_q, g_k]]
+    stream_tiles = [(0, TEXT_ROWS // P), (TEXT_ROWS // P, ROW_TILES)]
+    outs = [o.rearrange("b s h d -> (b s) (h d)") for o in (out_0, out_1)]
+    text = encoder_hidden_states.flatten_outer_dims()
+    image = hidden_states.flatten_outer_dims()
+    x_groups = [text] + [image[GROUP_ROWS * i : GROUP_ROWS * (i + 1), :] for i in range(GROUPS - 1)]
+
+    with ExitStack() as ctx:
+        keep = ctx.enter_context(tc.tile_pool(name="keep", bufs=1))
+        stage = ctx.enter_context(tc.tile_pool(name="stage", bufs=2))
+        work = ctx.enter_context(tc.tile_pool(name="work", bufs=4))
+        psum = ctx.enter_context(tc.psum_pool(name="psum", bufs=4))
+
+        x_rows = [keep.tile([P, GROUP_TILES, MODEL], BF16, name="x_rows%d" % g) for g in range(GROUPS)]
+        w_words = [
+            [keep.tile([P, PASSES, MODEL], U32, name="w_words%d%d" % (s, o), align_bytes=64) for o in range(2)]
+            for s in range(2)
+        ]
+        w_planes = [keep.tile([P, MODEL], U8, name="w_planes%d" % s, align_bytes=64) for s in range(2)]
+        for s in range(2):
+            nc.vector.memset(w_planes[s][:].bitcast(I32), 0)
+
+        def load_x(g):
+            nc.sync.dma_start(out=x_rows[g][:], in_=x_groups[g].rearrange("(j p) k -> p j k", p=P))
+
+        def load_weights(s):
+            for o in range(2):
+                for quad in range(4):
+                    first = 32 * quad + 8 * o
+                    nc.sync.dma_start(
+                        out=w_planes[s][first : first + 2 * PACK, :].bitcast(I32),
+                        in_=scales_in[s][o][:, 4 * quad : 4 * quad + 4, :].bitcast(I32),
+                    )
+            for o in range(2):
+                nc.sync.dma_start(
+                    out=w_words[s][o][:].bitcast(I32),
+                    in_=words_in[s][o].rearrange("g p n t -> p g (n t)").bitcast(I32),
+                )
+
+        load_x(0)
+        load_weights(0)
+        load_x(1)
+        load_weights(1)
+        load_x(2)
+        load_x(3)
+
+        bias_rows = keep.tile([P, P], BF16)
+        nc.vector.memset(bias_rows[:], 0.0)
+        for s in range(2):
+            for o in range(2):
+                first = HEADS * (2 * s + o)
+                nc.scalar.dma_start(
+                    out=bias_rows[first : first + HEADS, :], in_=bias_in[s][o].rearrange("(h d) -> h d", d=HEAD)
+                )
+        gain = [[keep.tile([P, HEAD], BF16, name="gain%d%d" % (s, o)) for o in range(2)] for s in range(2)]
+        for s in range(2):
+            for o in range(2):
+                nc.scalar.dma_start(out=gain[s][o][:], in_=gain_in[s][o].partition_broadcast(P))
+        cos = keep.tile([P, ROW_TILES, HEAD], BF16)
+        sin = keep.tile([P, ROW_TILES, HEAD], BF16)
+        nc.scalar.dma_start(out=cos[:], in_=rope_cos.rearrange("(t p) d -> p t d", p=P))
+        nc.scalar.dma_start(out=sin[:], in_=rope_sin.rearrange("(t p) d -> p t d", p=P))
+
+        ident = keep.tile([P, P], F32)
+        make_identity(nc, ident[:])
+        eps = keep.tile([P, 1], F32)
+        nc.vector.memset(eps[:], EPS)
+        table_warmer = keep.tile([P, 1], F32)
+        nc.scalar.activation(out=table_warmer[:], in_=eps[:], func=ACT.Sqrt)
+
+        table_a = [keep.tile([P, ROW_TILES, HEAD], F32, name="table_a%d" % o) for o in range(2)]
+        table_b = [keep.tile([P, ROW_TILES, 2, PAIRS], F32, name="table_b%d" % o) for o in range(2)]
+        for s in range(2):
+            t0, t1 = stream_tiles[s]
+            for o in range(2):
+                pairs = gain[s][o][:].rearrange("p (c e) -> p c e", e=2)
+                partner = keep.tile([P, 2, PAIRS], F32, name="partner%d%d" % (s, o))
+                nc.vector.tensor_scalar_mul(out=partner[:, 0, :], in0=pairs[:, :, 1], scalar1=-1.0)
+                nc.vector.tensor_copy(out=partner[:, 1, :], in_=pairs[:, :, 0])
+                nc.gpsimd.tensor_tensor(
+                    out=table_a[o][:, t0:t1, :],
+                    in0=cos[:, t0:t1, :],
+                    in1=gain[s][o][:].unsqueeze(1).to_broadcast([P, t1 - t0, HEAD]),
+                    op=ALU.mult,
+                )
+                nc.gpsimd.tensor_tensor(
+                    out=table_b[o][:, t0:t1, :, :],
+                    in0=sin[:, t0:t1, :].rearrange("p t (c e) -> p t e c", e=2),
+                    in1=partner[:].unsqueeze(1).to_broadcast([P, t1 - t0, 2, PAIRS]),
+                    op=ALU.mult,
+                )
+
+        x_codes = keep.tile([P, GROUPS, PASSES * GROUP_ROWS], U32, align_bytes=64)
+        x_scales = keep.tile([P, GROUPS, PASSES * GROUP_ROWS], U8, align_bytes=64)
+
+        def quantise_group(g):
+            grouped = stage.tile([P, PASSES * GROUP_ROWS * PACK], BF16, align_bytes=64)
+            halves = grouped[:].bitcast(F32).rearrange("p (g r u) -> p g r u", g=PASSES, u=2)
+            for j in range(GROUP_TILES):
+                words = x_rows[g][:, j, :].bitcast(F32)
+                flipped = psum.tile([P, PASSES * 2, P], F32, tag="acc")
+                for gu in range(PASSES * 2):
+                    first = (K_PASS // 2) * (gu // 2) + gu % 2
+                    last = (K_PASS // 2) * (gu // 2 + 1)
+                    nc.tensor.transpose(flipped[:, gu, :], words[:, first:last:2], ident[:])
+                copy = nc.vector.tensor_copy if j % 2 == 0 else nc.scalar.copy
+                copy(
+                    out=halves[:, :, P * j : P * (j + 1), :],
+                    in_=flipped[:].rearrange("p (g u) r -> p g r u", u=2),
+                )
+            nc.vector.quantize_mx(out=x_codes[:, g, :].bitcast(FP8X4), scales=x_scales[:, g, :], in_=grouped[:])
+
+        steps = [(g, o, half) for g in range(GROUPS) for o in range(2) for half in range(HEADS // STEP_HEADS)]
+        biased = {}
+        backs = {}
+        inv_rms = {}
+
+        def project(n):
+            g, o, half = steps[n]
+            s = min(g, 1)
+            biased[n] = work.tile([P, STEP_HEADS, GROUP_ROWS], F32, name="biased")
+            for b in range(STEP_HEADS // BANK_HEADS):
+                acc = psum.tile([P, BANK_HEADS, GROUP_ROWS], F32, tag="acc")
+                for i in range(BANK_HEADS):
+                    h = STEP_HEADS * half + BANK_HEADS * b + i
+                    cols = slice(HEAD * h, HEAD * (h + 1))
+                    for c in range(PASSES):
+                        rows = slice(GROUP_ROWS * c, GROUP_ROWS * (c + 1))
+                        nc.tensor.matmul_mx(
+                            out=acc[:, i, :],
+                            lhsT=w_words[s][o][:, c, cols].bitcast(FP8X4),
+                            lhsT_scale=w_planes[s][8 * o + 4 * c : P, cols],
+                            rhs=x_codes[:, g, rows].bitcast(FP8X4),
+                            rhs_scale=x_scales[:, g, rows],
+                            start=(c == 0),
+                            stop=(c == PASSES - 1),
+                        )
+                for i in range(BANK_HEADS):
+                    h = STEP_HEADS * half + BANK_HEADS * b + i
+                    col = HEADS * (2 * s + o) + h
+                    nc.scalar.activation(
+                        out=biased[n][:, BANK_HEADS * b + i, :],
+                        in_=acc[:, i, :],
+                        func=ACT.Identity,
+                        bias=bias_col[:, col : col + 1],
+                        scale=1.0,
+                    )
+
+        def norm(n):
+            sumsq = work.tile([P, GROUP_TILES * STEP_HEADS], F32, name="sumsq")
+            backs[n] = []
+            for j in range(GROUP_TILES):
+                back = psum.tile([P, STEP_HEADS, HEAD], F32, tag="back")
+                backs[n].append(back)
+                for i in range(STEP_HEADS):
+                    nc.tensor.transpose(back[:, i, :], biased[n][:, i, P * j : P * (j + 1)], ident[:])
+                for i in range(STEP_HEADS):
+                    squares = work.tile([P, HEAD], F32, name="squares")
+                    col = STEP_HEADS * j + i
+                    nc.scalar.activation(
+                        out=squares[:], in_=back[:, i, :], func=ACT.Square, accum_out=sumsq[:, col : col + 1]
+                    )
+            rms = work.tile([P, GROUP_TILES * STEP_HEADS], F32, name="rms")
+            nc.scalar.activation(out=rms[:], in_=sumsq[:], func=ACT.Sqrt, bias=eps[:, 0:1], scale=1.0 / HEAD)
+            inv_rms[n] = work.tile([P, GROUP_TILES * STEP_HEADS], F32, name="inv_rms")
+            nc.vector.reciprocal(out=inv_rms[n][:], in_=rms[:])
+
+        def rotate(n):
+            g, o, half = steps[n]
+            for j in range(GROUP_TILES):
+                t = GROUP_TILES * g + j
+                back = backs[n][j]
+                own = work.tile([P, STEP_HEADS, HEAD], F32, name="own")
+                other = work.tile([P, 2, STEP_HEADS, PAIRS], F32, name="other")
+                for i in range(STEP_HEADS):
+                    r = inv_rms[n][:, STEP_HEADS * j + i : STEP_HEADS * j + i + 1]
+                    nc.vector.scalar_tensor_tensor(
+                        out=own[:, i, :], in0=back[:, i, :], scalar=r, in1=table_a[o][:, t, :], op0=ALU.mult, op1=ALU.mult
+                    )
+                    pairs = back[:, i, :].rearrange("p (c e) -> p c e", e=2)
+                    for e in range(2):
+                        nc.vector.scalar_tensor_tensor(
+                            out=other[:, e, i, :],
+                            in0=pairs[:, :, 1 - e],
+                            scalar=r,
+                            in1=table_b[o][:, t, e, :],
+                            op0=ALU.mult,
+                            op1=ALU.mult,
+                        )
+                result = work.tile([P, STEP_HEADS * HEAD], F32, name="result")
+                nc.gpsimd.tensor_tensor(
+                    out=result[:].rearrange("p (n e) -> p n e", e=2),
+                    in0=own[:].rearrange("p h (c e) -> p (h c) e", e=2),
+                    in1=other[:].rearrange("p e h c -> p (h c) e"),
+                    op=ALU.add,
+                )
+                width = STEP_HEADS * HEAD
+                nc.sync.dma_start(out=outs[o][P * t : P * (t + 1), width * half : width * (half + 1)], in_=result[:])
+
+        quantise_group(0)
+
+        bias_rows32 = keep.tile([P, P], F32)
+        nc.vector.tensor_copy(out=bias_rows32[:], in_=bias_rows[:])
+        bias_ps = psum.tile([P, P], F32, tag="back")
+        nc.tensor.transpose(bias_ps[:], bias_rows32[:], ident[:])
+        bias_col = keep.tile([P, 4 * HEADS], F32)
+        nc.vector.tensor_copy(out=bias_col[:], in_=bias_ps[:, 0 : 4 * HEADS])
+
+        for n in range(len(steps) + 2):
+            if n < len(steps):
+                g, o, half = steps[n]
+                if (o, half) == (1, 0) and g + 1 < GROUPS:
+                    quantise_group(g + 1)
+                project(n)
+            if 1 <= n <= len(steps):
+                norm(n - 1)
+            if n >= 2:
+                rotate(n - 2)

@@ -76,6 +76,7 @@ def tile_fluxjointattention_pa_kernel(
         stage = ctx.enter_context(tc.tile_pool(name="stage", bufs=2))
         work = ctx.enter_context(tc.tile_pool(name="work", bufs=4))
         psum = ctx.enter_context(tc.psum_pool(name="psum", bufs=4))
+        ctx.enter_context(tc.manual_schedule())
 
         x_rows = [keep.tile([P, GROUP_TILES, MODEL], BF16, name="x_rows%d" % g) for g in range(GROUPS)]
         w_words = [
@@ -83,102 +84,118 @@ def tile_fluxjointattention_pa_kernel(
             for s in range(2)
         ]
         w_planes = [keep.tile([P, MODEL], U8, name="w_planes%d" % s, align_bytes=64) for s in range(2)]
+        bias_rows = [keep.tile([P, P], BF16, name="bias_rows%d" % s) for s in range(2)]
+        gain = [[keep.tile([P, HEAD], BF16, name="gain%d%d" % (s, o)) for o in range(2)] for s in range(2)]
+        cos = keep.tile([P, ROW_TILES, HEAD], BF16)
+        sin = keep.tile([P, ROW_TILES, HEAD], BF16)
         for s in range(2):
+            nc.vector.memset(bias_rows[s][:], 0.0)
             nc.vector.memset(w_planes[s][:].bitcast(I32), 0)
+        eps = keep.tile([P, 1], F32)
+        nc.vector.memset(eps[:], EPS)
+        ident = keep.tile([P, P], F32)
+        make_identity(nc, ident[:])
+        table_warmer = keep.tile([P, 1], F32)
+        nc.scalar.activation(out=table_warmer[:], in_=eps[:], func=ACT.Sqrt)
 
         def load_x(g):
             nc.sync.dma_start(out=x_rows[g][:], in_=x_groups[g].rearrange("(j p) k -> p j k", p=P))
 
-        def load_weights(s):
-            for o in range(2):
-                for quad in range(4):
-                    first = 32 * quad + 8 * o
-                    nc.sync.dma_start(
-                        out=w_planes[s][first : first + 2 * PACK, :].bitcast(I32),
-                        in_=scales_in[s][o][:, 4 * quad : 4 * quad + 4, :].bitcast(I32),
-                    )
+        def load_bias(s):
             for o in range(2):
                 nc.sync.dma_start(
-                    out=w_words[s][o][:].bitcast(I32),
-                    in_=words_in[s][o].rearrange("g p n t -> p g (n t)").bitcast(I32),
+                    out=bias_rows[s][HEADS * o : HEADS * (o + 1), :], in_=bias_in[s][o].rearrange("(h d) -> h d", d=HEAD)
                 )
 
+        def load_gain(s):
+            for o in range(2):
+                nc.sync.dma_start(out=gain[s][o][:], in_=gain_in[s][o].partition_broadcast(P))
+
+        def load_weight(s, o):
+            for quad in range(4):
+                first = 32 * quad + 8 * o
+                nc.sync.dma_start(
+                    out=w_planes[s][first : first + 2 * PACK, :].bitcast(I32),
+                    in_=scales_in[s][o][:, 4 * quad : 4 * quad + 4, :].bitcast(I32),
+                )
+            nc.sync.dma_start(
+                out=w_words[s][o][:].bitcast(I32),
+                in_=words_in[s][o].rearrange("g p n t -> p g (n t)").bitcast(I32),
+            )
+
         load_x(0)
-        load_weights(0)
+        load_bias(0)
+        load_weight(0, 0)
+        load_gain(0)
+        load_gain(1)
+        nc.sync.dma_start(out=cos[:], in_=rope_cos.rearrange("(t p) d -> p t d", p=P))
+        nc.sync.dma_start(out=sin[:], in_=rope_sin.rearrange("(t p) d -> p t d", p=P))
+        load_weight(0, 1)
         load_x(1)
-        load_weights(1)
+        load_bias(1)
+        load_weight(1, 0)
+        load_weight(1, 1)
         load_x(2)
         load_x(3)
 
-        bias_rows = keep.tile([P, P], BF16)
-        nc.vector.memset(bias_rows[:], 0.0)
-        for s in range(2):
-            for o in range(2):
-                first = HEADS * (2 * s + o)
-                nc.scalar.dma_start(
-                    out=bias_rows[first : first + HEADS, :], in_=bias_in[s][o].rearrange("(h d) -> h d", d=HEAD)
-                )
-        gain = [[keep.tile([P, HEAD], BF16, name="gain%d%d" % (s, o)) for o in range(2)] for s in range(2)]
-        for s in range(2):
-            for o in range(2):
-                nc.scalar.dma_start(out=gain[s][o][:], in_=gain_in[s][o].partition_broadcast(P))
-        cos = keep.tile([P, ROW_TILES, HEAD], BF16)
-        sin = keep.tile([P, ROW_TILES, HEAD], BF16)
-        nc.scalar.dma_start(out=cos[:], in_=rope_cos.rearrange("(t p) d -> p t d", p=P))
-        nc.scalar.dma_start(out=sin[:], in_=rope_sin.rearrange("(t p) d -> p t d", p=P))
-
-        ident = keep.tile([P, P], F32)
-        make_identity(nc, ident[:])
-        eps = keep.tile([P, 1], F32)
-        nc.vector.memset(eps[:], EPS)
-        table_warmer = keep.tile([P, 1], F32)
-        nc.scalar.activation(out=table_warmer[:], in_=eps[:], func=ACT.Sqrt)
-
+        bias_col = [keep.tile([P, 2 * HEADS], F32, name="bias_col%d" % s) for s in range(2)]
         table_a = [keep.tile([P, ROW_TILES, HEAD], F32, name="table_a%d" % o) for o in range(2)]
-        table_b = [keep.tile([P, ROW_TILES, 2, PAIRS], F32, name="table_b%d" % o) for o in range(2)]
-        for s in range(2):
+        table_b = [keep.tile([P, ROW_TILES, HEAD], F32, name="table_b%d" % o) for o in range(2)]
+
+        def bias_columns(s):
+            bias_rows32 = keep.tile([P, P], F32, name="bias_rows32_%d" % s)
+            nc.vector.tensor_copy(out=bias_rows32[:], in_=bias_rows[s][:])
+            bias_ps = psum.tile([P, P], F32, tag="acc")
+            nc.tensor.transpose(bias_ps[:], bias_rows32[:], ident[:])
+            nc.vector.tensor_copy(out=bias_col[s][:], in_=bias_ps[:, 0 : 2 * HEADS])
+
+        def tables(s):
             t0, t1 = stream_tiles[s]
             for o in range(2):
-                pairs = gain[s][o][:].rearrange("p (c e) -> p c e", e=2)
-                partner = keep.tile([P, 2, PAIRS], F32, name="partner%d%d" % (s, o))
-                nc.vector.tensor_scalar_mul(out=partner[:, 0, :], in0=pairs[:, :, 1], scalar1=-1.0)
-                nc.vector.tensor_copy(out=partner[:, 1, :], in_=pairs[:, :, 0])
                 nc.gpsimd.tensor_tensor(
                     out=table_a[o][:, t0:t1, :],
                     in0=cos[:, t0:t1, :],
                     in1=gain[s][o][:].unsqueeze(1).to_broadcast([P, t1 - t0, HEAD]),
                     op=ALU.mult,
                 )
-                nc.gpsimd.tensor_tensor(
-                    out=table_b[o][:, t0:t1, :, :],
-                    in0=sin[:, t0:t1, :].rearrange("p t (c e) -> p t e c", e=2),
-                    in1=partner[:].unsqueeze(1).to_broadcast([P, t1 - t0, 2, PAIRS]),
+                gain_pairs = gain[s][o][:].rearrange("p (c e) -> p c e", e=2)
+                partner = keep.tile([P, PAIRS, 2], F32, name="partner%d%d" % (s, o))
+                nc.vector.tensor_scalar_mul(out=partner[:, :, 0], in0=gain_pairs[:, :, 1], scalar1=-1.0)
+                nc.vector.tensor_copy(out=partner[:, :, 1], in_=gain_pairs[:, :, 0])
+                nc.vector.tensor_tensor(
+                    out=table_b[o][:, t0:t1, :],
+                    in0=sin[:, t0:t1, :],
+                    in1=partner[:].rearrange("p c e -> p (c e)").unsqueeze(1).to_broadcast([P, t1 - t0, HEAD]),
                     op=ALU.mult,
                 )
 
         x_codes = keep.tile([P, GROUPS, PASSES * GROUP_ROWS], U32, align_bytes=64)
         x_scales = keep.tile([P, GROUPS, PASSES * GROUP_ROWS], U8, align_bytes=64)
+        grouped = {}
 
-        def quantise_group(g):
-            grouped = stage.tile([P, PASSES * GROUP_ROWS * PACK], BF16, align_bytes=64)
-            halves = grouped[:].bitcast(F32).rearrange("p (g r u) -> p g r u", g=PASSES, u=2)
+        def flip_group(g):
+            grouped[g] = stage.tile([P, PASSES * GROUP_ROWS * PACK], BF16, name="grouped", align_bytes=64)
+            halves = grouped[g][:].bitcast(F32).rearrange("p (c r u) -> p c r u", c=PASSES, u=2)
             for j in range(GROUP_TILES):
                 words = x_rows[g][:, j, :].bitcast(F32)
                 flipped = psum.tile([P, PASSES * 2, P], F32, tag="acc")
-                for gu in range(PASSES * 2):
-                    first = (K_PASS // 2) * (gu // 2) + gu % 2
-                    last = (K_PASS // 2) * (gu // 2 + 1)
-                    nc.tensor.transpose(flipped[:, gu, :], words[:, first:last:2], ident[:])
+                for cu in range(PASSES * 2):
+                    first = (K_PASS // 2) * (cu // 2) + cu % 2
+                    last = (K_PASS // 2) * (cu // 2 + 1)
+                    nc.tensor.transpose(flipped[:, cu, :], words[:, first:last:2], ident[:])
                 copy = nc.vector.tensor_copy if j % 2 == 0 else nc.scalar.copy
                 copy(
                     out=halves[:, :, P * j : P * (j + 1), :],
-                    in_=flipped[:].rearrange("p (g u) r -> p g r u", u=2),
+                    in_=flipped[:].rearrange("p (c u) r -> p c r u", u=2),
                 )
-            nc.vector.quantize_mx(out=x_codes[:, g, :].bitcast(FP8X4), scales=x_scales[:, g, :], in_=grouped[:])
+
+        def quantise_group(g):
+            nc.vector.quantize_mx(out=x_codes[:, g, :].bitcast(FP8X4), scales=x_scales[:, g, :], in_=grouped[g][:])
 
         steps = [(g, o, half) for g in range(GROUPS) for o in range(2) for half in range(HEADS // STEP_HEADS)]
         biased = {}
         backs = {}
+        rms = {}
         inv_rms = {}
 
         def project(n):
@@ -202,17 +219,16 @@ def tile_fluxjointattention_pa_kernel(
                             stop=(c == PASSES - 1),
                         )
                 for i in range(BANK_HEADS):
-                    h = STEP_HEADS * half + BANK_HEADS * b + i
-                    col = HEADS * (2 * s + o) + h
+                    col = HEADS * o + STEP_HEADS * half + BANK_HEADS * b + i
                     nc.scalar.activation(
                         out=biased[n][:, BANK_HEADS * b + i, :],
                         in_=acc[:, i, :],
                         func=ACT.Identity,
-                        bias=bias_col[:, col : col + 1],
+                        bias=bias_col[s][:, col : col + 1],
                         scale=1.0,
                     )
 
-        def norm(n):
+        def measure(n):
             sumsq = work.tile([P, GROUP_TILES * STEP_HEADS], F32, name="sumsq")
             backs[n] = []
             for j in range(GROUP_TILES):
@@ -226,10 +242,12 @@ def tile_fluxjointattention_pa_kernel(
                     nc.scalar.activation(
                         out=squares[:], in_=back[:, i, :], func=ACT.Square, accum_out=sumsq[:, col : col + 1]
                     )
-            rms = work.tile([P, GROUP_TILES * STEP_HEADS], F32, name="rms")
-            nc.scalar.activation(out=rms[:], in_=sumsq[:], func=ACT.Sqrt, bias=eps[:, 0:1], scale=1.0 / HEAD)
+            rms[n] = work.tile([P, GROUP_TILES * STEP_HEADS], F32, name="rms")
+            nc.scalar.activation(out=rms[n][:], in_=sumsq[:], func=ACT.Sqrt, bias=eps[:, 0:1], scale=1.0 / HEAD)
+
+        def invert(n):
             inv_rms[n] = work.tile([P, GROUP_TILES * STEP_HEADS], F32, name="inv_rms")
-            nc.vector.reciprocal(out=inv_rms[n][:], in_=rms[:])
+            nc.vector.reciprocal(out=inv_rms[n][:], in_=rms[n][:])
 
         def rotate(n):
             g, o, half = steps[n]
@@ -237,48 +255,48 @@ def tile_fluxjointattention_pa_kernel(
                 t = GROUP_TILES * g + j
                 back = backs[n][j]
                 own = work.tile([P, STEP_HEADS, HEAD], F32, name="own")
-                other = work.tile([P, 2, STEP_HEADS, PAIRS], F32, name="other")
+                other = work.tile([P, STEP_HEADS, HEAD], F32, name="other")
                 for i in range(STEP_HEADS):
                     r = inv_rms[n][:, STEP_HEADS * j + i : STEP_HEADS * j + i + 1]
                     nc.vector.scalar_tensor_tensor(
                         out=own[:, i, :], in0=back[:, i, :], scalar=r, in1=table_a[o][:, t, :], op0=ALU.mult, op1=ALU.mult
                     )
-                    pairs = back[:, i, :].rearrange("p (c e) -> p c e", e=2)
-                    for e in range(2):
-                        nc.vector.scalar_tensor_tensor(
-                            out=other[:, e, i, :],
-                            in0=pairs[:, :, 1 - e],
-                            scalar=r,
-                            in1=table_b[o][:, t, e, :],
-                            op0=ALU.mult,
-                            op1=ALU.mult,
-                        )
+                    nc.vector.scalar_tensor_tensor(
+                        out=other[:, i, :].rearrange("p (c e) -> p c e", e=2),
+                        in0=back[:, i, :].rearrange("p (c e) -> p c e", e=2)[:, :, ::-1],
+                        scalar=r,
+                        in1=table_b[o][:, t, :].rearrange("p (c e) -> p c e", e=2),
+                        op0=ALU.mult,
+                        op1=ALU.mult,
+                    )
                 result = work.tile([P, STEP_HEADS * HEAD], F32, name="result")
                 nc.gpsimd.tensor_tensor(
-                    out=result[:].rearrange("p (n e) -> p n e", e=2),
-                    in0=own[:].rearrange("p h (c e) -> p (h c) e", e=2),
-                    in1=other[:].rearrange("p e h c -> p (h c) e"),
+                    out=result[:],
+                    in0=own[:].rearrange("p h d -> p (h d)"),
+                    in1=other[:].rearrange("p h d -> p (h d)"),
                     op=ALU.add,
                 )
                 width = STEP_HEADS * HEAD
                 nc.sync.dma_start(out=outs[o][P * t : P * (t + 1), width * half : width * (half + 1)], in_=result[:])
 
+        bias_columns(0)
+        flip_group(0)
         quantise_group(0)
-
-        bias_rows32 = keep.tile([P, P], F32)
-        nc.vector.tensor_copy(out=bias_rows32[:], in_=bias_rows[:])
-        bias_ps = psum.tile([P, P], F32, tag="back")
-        nc.tensor.transpose(bias_ps[:], bias_rows32[:], ident[:])
-        bias_col = keep.tile([P, 4 * HEADS], F32)
-        nc.vector.tensor_copy(out=bias_col[:], in_=bias_ps[:, 0 : 4 * HEADS])
-
+        tables(0)
+        tables(1)
         for n in range(len(steps) + 2):
+            next_group = n // 4 + 1 if n % 4 == 2 and n // 4 + 1 < GROUPS else None
+            if next_group is not None:
+                flip_group(next_group)
             if n < len(steps):
-                g, o, half = steps[n]
-                if (o, half) == (1, 0) and g + 1 < GROUPS:
-                    quantise_group(g + 1)
                 project(n)
             if 1 <= n <= len(steps):
-                norm(n - 1)
+                measure(n - 1)
             if n >= 2:
                 rotate(n - 2)
+            if next_group is not None:
+                quantise_group(next_group)
+            if next_group == 1:
+                bias_columns(1)
+            if 1 <= n <= len(steps):
+                invert(n - 1)

@@ -195,55 +195,58 @@ def tile_fluxjointattention_pa_kernel(
         steps = [(g, o, half) for g in range(GROUPS) for o in range(2) for half in range(HEADS // STEP_HEADS)]
         biased = {}
         backs = {}
+        sumsq = {}
         rms = {}
         inv_rms = {}
 
-        def project(n):
+        def project(n, b):
             g, o, half = steps[n]
             s = min(g, 1)
-            biased[n] = work.tile([P, STEP_HEADS, GROUP_ROWS], F32, name="biased")
-            for b in range(STEP_HEADS // BANK_HEADS):
-                acc = psum.tile([P, BANK_HEADS, GROUP_ROWS], F32, tag="acc")
-                for i in range(BANK_HEADS):
-                    h = STEP_HEADS * half + BANK_HEADS * b + i
-                    cols = slice(HEAD * h, HEAD * (h + 1))
-                    for c in range(PASSES):
-                        rows = slice(GROUP_ROWS * c, GROUP_ROWS * (c + 1))
-                        nc.tensor.matmul_mx(
-                            out=acc[:, i, :],
-                            lhsT=w_words[s][o][:, c, cols].bitcast(FP8X4),
-                            lhsT_scale=w_planes[s][8 * o + 4 * c : P, cols],
-                            rhs=x_codes[:, g, rows].bitcast(FP8X4),
-                            rhs_scale=x_scales[:, g, rows],
-                            start=(c == 0),
-                            stop=(c == PASSES - 1),
-                        )
-                for i in range(BANK_HEADS):
-                    col = HEADS * o + STEP_HEADS * half + BANK_HEADS * b + i
-                    nc.scalar.activation(
-                        out=biased[n][:, BANK_HEADS * b + i, :],
-                        in_=acc[:, i, :],
-                        func=ACT.Identity,
-                        bias=bias_col[s][:, col : col + 1],
-                        scale=1.0,
+            if b == 0:
+                biased[n] = work.tile([P, STEP_HEADS, GROUP_ROWS], F32, name="biased")
+            acc = psum.tile([P, BANK_HEADS, GROUP_ROWS], F32, tag="acc")
+            for i in range(BANK_HEADS):
+                h = STEP_HEADS * half + BANK_HEADS * b + i
+                cols = slice(HEAD * h, HEAD * (h + 1))
+                for c in range(PASSES):
+                    rows = slice(GROUP_ROWS * c, GROUP_ROWS * (c + 1))
+                    nc.tensor.matmul_mx(
+                        out=acc[:, i, :],
+                        lhsT=w_words[s][o][:, c, cols].bitcast(FP8X4),
+                        lhsT_scale=w_planes[s][8 * o + 4 * c : P, cols],
+                        rhs=x_codes[:, g, rows].bitcast(FP8X4),
+                        rhs_scale=x_scales[:, g, rows],
+                        start=(c == 0),
+                        stop=(c == PASSES - 1),
                     )
+            for i in range(BANK_HEADS):
+                col = HEADS * o + STEP_HEADS * half + BANK_HEADS * b + i
+                nc.scalar.activation(
+                    out=biased[n][:, BANK_HEADS * b + i, :],
+                    in_=acc[:, i, :],
+                    func=ACT.Identity,
+                    bias=bias_col[s][:, col : col + 1],
+                    scale=1.0,
+                )
 
-        def measure(n):
-            sumsq = work.tile([P, GROUP_TILES * STEP_HEADS], F32, name="sumsq")
-            backs[n] = []
-            for j in range(GROUP_TILES):
-                back = psum.tile([P, STEP_HEADS, HEAD], F32, tag="back")
-                backs[n].append(back)
-                for i in range(STEP_HEADS):
-                    nc.tensor.transpose(back[:, i, :], biased[n][:, i, P * j : P * (j + 1)], ident[:])
-                for i in range(STEP_HEADS):
-                    squares = work.tile([P, HEAD], F32, name="squares")
-                    col = STEP_HEADS * j + i
-                    nc.scalar.activation(
-                        out=squares[:], in_=back[:, i, :], func=ACT.Square, accum_out=sumsq[:, col : col + 1]
-                    )
+        def measure(n, j):
+            if j == 0:
+                sumsq[n] = work.tile([P, GROUP_TILES * STEP_HEADS], F32, name="sumsq")
+                backs[n] = []
+            back = psum.tile([P, STEP_HEADS, HEAD], F32, tag="back")
+            backs[n].append(back)
+            for i in range(STEP_HEADS):
+                nc.tensor.transpose(back[:, i, :], biased[n][:, i, P * j : P * (j + 1)], ident[:])
+            for i in range(STEP_HEADS):
+                squares = work.tile([P, HEAD], F32, name="squares")
+                col = STEP_HEADS * j + i
+                nc.scalar.activation(
+                    out=squares[:], in_=back[:, i, :], func=ACT.Square, accum_out=sumsq[n][:, col : col + 1]
+                )
+
+        def root(n):
             rms[n] = work.tile([P, GROUP_TILES * STEP_HEADS], F32, name="rms")
-            nc.scalar.activation(out=rms[n][:], in_=sumsq[:], func=ACT.Sqrt, bias=eps[:, 0:1], scale=1.0 / HEAD)
+            nc.scalar.activation(out=rms[n][:], in_=sumsq[n][:], func=ACT.Sqrt, bias=eps[:, 0:1], scale=1.0 / HEAD)
 
         def invert(n):
             inv_rms[n] = work.tile([P, GROUP_TILES * STEP_HEADS], F32, name="inv_rms")
@@ -288,10 +291,13 @@ def tile_fluxjointattention_pa_kernel(
             next_group = n // 4 + 1 if n % 4 == 2 and n // 4 + 1 < GROUPS else None
             if next_group is not None:
                 flip_group(next_group)
-            if n < len(steps):
-                project(n)
+            for part in range(2):
+                if n < len(steps):
+                    project(n, part)
+                if 1 <= n <= len(steps):
+                    measure(n - 1, part)
             if 1 <= n <= len(steps):
-                measure(n - 1)
+                root(n - 1)
             if n >= 2:
                 rotate(n - 2)
             if next_group is not None:

@@ -139,8 +139,7 @@ def tile_fluxjointattention_pa_kernel(
         load_x(3)
 
         bias_col = [keep.tile([P, 2 * HEADS], F32, name="bias_col%d" % s) for s in range(2)]
-        table_a = [keep.tile([P, ROW_TILES, HEAD], F32, name="table_a%d" % o) for o in range(2)]
-        table_b = [keep.tile([P, ROW_TILES, HEAD], F32, name="table_b%d" % o) for o in range(2)]
+        table = [keep.tile([P, ROW_TILES, 2, HEAD], F32, name="table%d" % o) for o in range(2)]
 
         def bias_columns(s):
             bias_rows32 = keep.tile([P, P], F32, name="bias_rows32_%d" % s)
@@ -153,19 +152,19 @@ def tile_fluxjointattention_pa_kernel(
             t0, t1 = stream_tiles[s]
             for o in range(2):
                 nc.gpsimd.tensor_tensor(
-                    out=table_a[o][:, t0:t1, :],
+                    out=table[o][:, t0:t1, 0, :],
                     in0=cos[:, t0:t1, :],
                     in1=gain[s][o][:].unsqueeze(1).to_broadcast([P, t1 - t0, HEAD]),
                     op=ALU.mult,
                 )
                 gain_pairs = gain[s][o][:].rearrange("p (c e) -> p c e", e=2)
-                partner = keep.tile([P, PAIRS, 2], F32, name="partner%d%d" % (s, o))
-                nc.vector.tensor_scalar_mul(out=partner[:, :, 0], in0=gain_pairs[:, :, 1], scalar1=-1.0)
-                nc.vector.tensor_copy(out=partner[:, :, 1], in_=gain_pairs[:, :, 0])
+                signed = keep.tile([P, PAIRS, 2], F32, name="signed%d%d" % (s, o))
+                nc.vector.tensor_copy(out=signed[:, :, 0], in_=gain_pairs[:, :, 0])
+                nc.vector.tensor_scalar_mul(out=signed[:, :, 1], in0=gain_pairs[:, :, 1], scalar1=-1.0)
                 nc.vector.tensor_tensor(
-                    out=table_b[o][:, t0:t1, :],
-                    in0=sin[:, t0:t1, :],
-                    in1=partner[:].rearrange("p c e -> p (c e)").unsqueeze(1).to_broadcast([P, t1 - t0, HEAD]),
+                    out=table[o][:, t0:t1, 1, :].rearrange("p t (c e) -> p t c e", e=2),
+                    in0=sin[:, t0:t1, :].rearrange("p t (c e) -> p t c e", e=2)[:, :, :, ::-1],
+                    in1=signed[:].unsqueeze(1).to_broadcast([P, t1 - t0, PAIRS, 2]),
                     op=ALU.mult,
                 )
 
@@ -257,30 +256,29 @@ def tile_fluxjointattention_pa_kernel(
             for j in range(GROUP_TILES):
                 t = GROUP_TILES * g + j
                 back = backs[n][j]
-                own = work.tile([P, STEP_HEADS, HEAD], F32, name="own")
-                other = work.tile([P, STEP_HEADS, HEAD], F32, name="other")
+                products = work.tile([P, STEP_HEADS, 2, HEAD], F32, name="products")
                 for i in range(STEP_HEADS):
                     r = inv_rms[n][:, STEP_HEADS * j + i : STEP_HEADS * j + i + 1]
                     nc.vector.scalar_tensor_tensor(
-                        out=own[:, i, :], in0=back[:, i, :], scalar=r, in1=table_a[o][:, t, :], op0=ALU.mult, op1=ALU.mult
-                    )
-                    nc.vector.scalar_tensor_tensor(
-                        out=other[:, i, :].rearrange("p (c e) -> p c e", e=2),
-                        in0=back[:, i, :].rearrange("p (c e) -> p c e", e=2)[:, :, ::-1],
+                        out=products[:, i, :, :],
+                        in0=back[:, i, :].unsqueeze(1).to_broadcast([P, 2, HEAD]),
                         scalar=r,
-                        in1=table_b[o][:, t, :].rearrange("p (c e) -> p c e", e=2),
+                        in1=table[o][:, t, :, :],
                         op0=ALU.mult,
                         op1=ALU.mult,
                     )
-                result = work.tile([P, STEP_HEADS * HEAD], F32, name="result")
+                result = work.tile([P, STEP_HEADS, PAIRS, 2], F32, name="result")
                 nc.gpsimd.tensor_tensor(
                     out=result[:],
-                    in0=own[:].rearrange("p h d -> p (h d)"),
-                    in1=other[:].rearrange("p h d -> p (h d)"),
+                    in0=products[:, :, 0, :].rearrange("p h (c e) -> p h c e", e=2),
+                    in1=products[:, :, 1, :].rearrange("p h (c e) -> p h c e", e=2)[:, :, :, ::-1],
                     op=ALU.add,
                 )
                 width = STEP_HEADS * HEAD
-                nc.sync.dma_start(out=outs[o][P * t : P * (t + 1), width * half : width * (half + 1)], in_=result[:])
+                nc.sync.dma_start(
+                    out=outs[o][P * t : P * (t + 1), width * half : width * (half + 1)],
+                    in_=result[:].rearrange("p h c e -> p (h c e)"),
+                )
 
         bias_columns(0)
         flip_group(0)

@@ -96,7 +96,7 @@ def tile_fluxjointattention_pa_kernel(
         ident = keep.tile([P, P], F32)
         make_identity(nc, ident[:])
         table_warmer = keep.tile([P, 1], F32)
-        nc.scalar.activation(out=table_warmer[:], in_=eps[:], func=ACT.Sqrt)
+        nc.scalar.activation(out=table_warmer[:], in_=eps[:], func=ACT.Abs_reciprocal_sqrt)
 
         def load_x(g):
             nc.sync.dma_start(out=x_rows[g][:], in_=x_groups[g].rearrange("(j p) k -> p j k", p=P))
@@ -244,12 +244,10 @@ def tile_fluxjointattention_pa_kernel(
                 )
 
         def root(n):
-            rms[n] = work.tile([P, GROUP_TILES * STEP_HEADS], F32, name="rms")
-            nc.scalar.activation(out=rms[n][:], in_=sumsq[n][:], func=ACT.Sqrt, bias=eps[:, 0:1], scale=1.0 / HEAD)
-
-        def invert(n):
             inv_rms[n] = work.tile([P, GROUP_TILES * STEP_HEADS], F32, name="inv_rms")
-            nc.vector.reciprocal(out=inv_rms[n][:], in_=rms[n][:])
+            nc.scalar.activation(
+                out=inv_rms[n][:], in_=sumsq[n][:], func=ACT.Abs_reciprocal_sqrt, bias=eps[:, 0:1], scale=1.0 / HEAD
+            )
 
         def rotate(n):
             g, o, half = steps[n]
@@ -302,5 +300,3 @@ def tile_fluxjointattention_pa_kernel(
                 quantise_group(next_group)
             if next_group == 1:
                 bias_columns(1)
-            if 1 <= n <= len(steps):
-                invert(n - 1)

@@ -78,19 +78,30 @@ def tile_fluxjointattention_pa_kernel(
         psum = ctx.enter_context(tc.psum_pool(name="psum", bufs=4))
         ctx.enter_context(tc.manual_schedule())
 
-        x_rows = [keep.tile([P, GROUP_TILES, MODEL], BF16, name="x_rows%d" % g) for g in range(GROUPS)]
+        x_rows = [
+            [keep.tile([P, MODEL], BF16, name="x_rows%d%d" % (g, j)) for j in range(GROUP_TILES)] for g in range(GROUPS)
+        ]
         w_words = [
-            [keep.tile([P, PASSES, MODEL], U32, name="w_words%d%d" % (s, o), align_bytes=64) for o in range(2)]
+            [
+                [
+                    keep.tile([P, PASSES, STEP_HEADS * HEAD], U32, name="w_words%d%d%d" % (s, o, half), align_bytes=64)
+                    for half in range(HEADS // STEP_HEADS)
+                ]
+                for o in range(2)
+            ]
             for s in range(2)
         ]
-        w_planes = [keep.tile([P, MODEL], U8, name="w_planes%d" % s, align_bytes=64) for s in range(2)]
+        w_planes = [
+            [keep.tile([P, MODEL], U8, name="w_planes%d%d" % (s, o), align_bytes=64) for o in range(2)] for s in range(2)
+        ]
         bias_rows = [keep.tile([P, P], BF16, name="bias_rows%d" % s) for s in range(2)]
         gain = [[keep.tile([P, HEAD], BF16, name="gain%d%d" % (s, o)) for o in range(2)] for s in range(2)]
         cos = keep.tile([P, ROW_TILES, HEAD], BF16)
         sin = keep.tile([P, ROW_TILES, HEAD], BF16)
         for s in range(2):
             nc.vector.memset(bias_rows[s][:], 0.0)
-            nc.vector.memset(w_planes[s][:].bitcast(I32), 0)
+            for o in range(2):
+                nc.vector.memset(w_planes[s][o][:].bitcast(I32), 0)
         eps = keep.tile([P, 1], F32)
         nc.vector.memset(eps[:], EPS)
         ident = keep.tile([P, P], F32)
@@ -99,7 +110,8 @@ def tile_fluxjointattention_pa_kernel(
         nc.scalar.activation(out=table_warmer[:], in_=eps[:], func=ACT.Abs_reciprocal_sqrt)
 
         def load_x(g):
-            nc.sync.dma_start(out=x_rows[g][:], in_=x_groups[g].rearrange("(j p) k -> p j k", p=P))
+            for j in range(GROUP_TILES):
+                nc.sync.dma_start(out=x_rows[g][j][:], in_=x_groups[g][P * j : P * (j + 1), :])
 
         def load_bias(s):
             for o in range(2):
@@ -111,21 +123,31 @@ def tile_fluxjointattention_pa_kernel(
             for o in range(2):
                 nc.sync.dma_start(out=gain[s][o][:], in_=gain_in[s][o].partition_broadcast(P))
 
-        def load_weight(s, o):
+        def load_scales(s, o):
             for quad in range(4):
-                first = 32 * quad + 8 * o
+                first = 32 * quad
                 nc.sync.dma_start(
-                    out=w_planes[s][first : first + 2 * PACK, :].bitcast(I32),
+                    out=w_planes[s][o][first : first + 2 * PACK, :].bitcast(I32),
                     in_=scales_in[s][o][:, 4 * quad : 4 * quad + 4, :].bitcast(I32),
                 )
+
+        def load_words(s, o, half):
+            width = STEP_HEADS * HEAD * PACK
             nc.sync.dma_start(
-                out=w_words[s][o][:].bitcast(I32),
-                in_=words_in[s][o].rearrange("g p n t -> p g (n t)").bitcast(I32),
+                out=w_words[s][o][half][:].bitcast(I32),
+                in_=words_in[s][o].rearrange("g p n t -> p g (n t)")[:, :, width * half : width * (half + 1)].bitcast(I32),
             )
 
+        def load_weight(s, o):
+            load_scales(s, o)
+            for half in range(HEADS // STEP_HEADS):
+                load_words(s, o, half)
+
         load_x(0)
+        load_scales(0, 0)
+        load_words(0, 0, 0)
         load_bias(0)
-        load_weight(0, 0)
+        load_words(0, 0, 1)
         load_gain(0)
         load_gain(1)
         nc.sync.dma_start(out=cos[:], in_=rope_cos.rearrange("(t p) d -> p t d", p=P))
@@ -176,7 +198,7 @@ def tile_fluxjointattention_pa_kernel(
             grouped[g] = stage.tile([P, PASSES * GROUP_ROWS * PACK], BF16, name="grouped", align_bytes=64)
             halves = grouped[g][:].bitcast(F32).rearrange("p (c r u) -> p c r u", c=PASSES, u=2)
             for j in range(GROUP_TILES):
-                words = x_rows[g][:, j, :].bitcast(F32)
+                words = x_rows[g][j][:].bitcast(F32)
                 flipped = psum.tile([P, PASSES * 2, P], F32, tag="acc")
                 for cu in range(PASSES * 2):
                     first = (K_PASS // 2) * (cu // 2) + cu % 2
@@ -207,12 +229,13 @@ def tile_fluxjointattention_pa_kernel(
             for i in range(BANK_HEADS):
                 h = STEP_HEADS * half + BANK_HEADS * b + i
                 cols = slice(HEAD * h, HEAD * (h + 1))
+                own_cols = slice(HEAD * (BANK_HEADS * b + i), HEAD * (BANK_HEADS * b + i + 1))
                 for c in range(PASSES):
                     rows = slice(GROUP_ROWS * c, GROUP_ROWS * (c + 1))
                     nc.tensor.matmul_mx(
                         out=acc[:, i, :],
-                        lhsT=w_words[s][o][:, c, cols].bitcast(FP8X4),
-                        lhsT_scale=w_planes[s][8 * o + 4 * c : P, cols],
+                        lhsT=w_words[s][o][half][:, c, own_cols].bitcast(FP8X4),
+                        lhsT_scale=w_planes[s][o][4 * c : P, cols],
                         rhs=x_codes[:, g, rows].bitcast(FP8X4),
                         rhs_scale=x_scales[:, g, rows],
                         start=(c == 0),
@@ -278,8 +301,8 @@ def tile_fluxjointattention_pa_kernel(
                     in_=result[:].rearrange("p h c e -> p (h c e)"),
                 )
 
-        bias_columns(0)
         flip_group(0)
+        bias_columns(0)
         quantise_group(0)
         tables(0)
         tables(1)

@@ -30,6 +30,7 @@ GROUP_TILES = GROUP_ROWS // P
 ROW_TILES = SEQ // P
 STEP_HEADS = 4
 BANK_HEADS = 2
+VECTOR_STEP_PERIOD = 4
 
 FLOPS = 2 * SEQ * MODEL * 2 * MODEL
 
@@ -214,6 +215,7 @@ def tile_fluxjointattention_pa_kernel(
             nc.vector.quantize_mx(out=x_codes[:, g, :].bitcast(FP8X4), scales=x_scales[:, g, :], in_=grouped[g][:])
 
         steps = [(g, o, half) for g in range(GROUPS) for o in range(2) for half in range(HEADS // STEP_HEADS)]
+        accs = {}
         biased = {}
         backs = {}
         sumsq = {}
@@ -226,6 +228,7 @@ def tile_fluxjointattention_pa_kernel(
             if b == 0:
                 biased[n] = work.tile([P, STEP_HEADS, GROUP_ROWS], F32, name="biased")
             acc = psum.tile([P, BANK_HEADS, GROUP_ROWS], F32, tag="acc")
+            accs[n, b] = acc
             for i in range(BANK_HEADS):
                 h = STEP_HEADS * half + BANK_HEADS * b + i
                 cols = slice(HEAD * h, HEAD * (h + 1))
@@ -241,15 +244,31 @@ def tile_fluxjointattention_pa_kernel(
                         start=(c == 0),
                         stop=(c == PASSES - 1),
                     )
+            if not on_vector(n, b):
+                add_bias(n, b)
+
+        def on_vector(n, b):
+            return b == 1 and n % VECTOR_STEP_PERIOD == VECTOR_STEP_PERIOD - 1
+
+        def add_bias(n, b):
+            g, o, half = steps[n]
+            s = min(g, 1)
             for i in range(BANK_HEADS):
                 col = HEADS * o + STEP_HEADS * half + BANK_HEADS * b + i
-                nc.scalar.activation(
-                    out=biased[n][:, BANK_HEADS * b + i, :],
-                    in_=acc[:, i, :],
-                    func=ACT.Identity,
-                    bias=bias_col[s][:, col : col + 1],
-                    scale=1.0,
-                )
+                if on_vector(n, b):
+                    nc.vector.tensor_scalar_add(
+                        out=biased[n][:, BANK_HEADS * b + i, :],
+                        in0=accs[n, b][:, i, :],
+                        scalar1=bias_col[s][:, col : col + 1],
+                    )
+                else:
+                    nc.scalar.activation(
+                        out=biased[n][:, BANK_HEADS * b + i, :],
+                        in_=accs[n, b][:, i, :],
+                        func=ACT.Identity,
+                        bias=bias_col[s][:, col : col + 1],
+                        scale=1.0,
+                    )
 
         def measure(n, j):
             if j == 0:
@@ -272,9 +291,11 @@ def tile_fluxjointattention_pa_kernel(
                 out=inv_rms[n][:], in_=sumsq[n][:], func=ACT.Abs_reciprocal_sqrt, bias=eps[:, 0:1], scale=1.0 / HEAD
             )
 
-        def rotate(n):
+        def rotate(n, between):
             g, o, half = steps[n]
             for j in range(GROUP_TILES):
+                if j == 1 and between is not None:
+                    add_bias(between, 1)
                 t = GROUP_TILES * g + j
                 back = backs[n][j]
                 products = work.tile([P, STEP_HEADS, 2, HEAD], F32, name="products")
@@ -318,7 +339,7 @@ def tile_fluxjointattention_pa_kernel(
             if 1 <= n <= len(steps):
                 root(n - 1)
             if n >= 2:
-                rotate(n - 2)
+                rotate(n - 2, n if n < len(steps) and on_vector(n, 1) else None)
             if next_group is not None:
                 quantise_group(next_group)
             if next_group == 1:

@@ -310,7 +310,8 @@ def tile_fluxjointattention_pa_kernel(
                         op1=ALU.mult,
                     )
                 result = work.tile([P, STEP_HEADS, PAIRS, 2], F32, name="result")
-                nc.gpsimd.tensor_tensor(
+                adder = nc.vector if (n, j) == (len(steps) - 1, GROUP_TILES - 1) else nc.gpsimd
+                adder.tensor_tensor(
                     out=result[:],
                     in0=products[:, :, 0, :].rearrange("p h (c e) -> p h c e", e=2),
                     in1=products[:, :, 1, :].rearrange("p h (c e) -> p h c e", e=2)[:, :, :, ::-1],

@@ -75,8 +75,9 @@ def tile_fluxjointattention_pa_kernel(
     with ExitStack() as ctx:
         keep = ctx.enter_context(tc.tile_pool(name="keep", bufs=1))
         stage = ctx.enter_context(tc.tile_pool(name="stage", bufs=2))
-        work = ctx.enter_context(tc.tile_pool(name="work", bufs=4))
-        psum = ctx.enter_context(tc.psum_pool(name="psum", bufs=4))
+        work = ctx.enter_context(tc.tile_pool(name="work", bufs=6))
+        psum = ctx.enter_context(tc.psum_pool(name="psum", bufs=3))
+        psum_back = ctx.enter_context(tc.psum_pool(name="psum_back", bufs=5))
         ctx.enter_context(tc.manual_schedule())
 
         x_rows = [
@@ -274,7 +275,7 @@ def tile_fluxjointattention_pa_kernel(
             if j == 0:
                 sumsq[n] = work.tile([P, GROUP_TILES * STEP_HEADS], F32, name="sumsq")
                 backs[n] = []
-            back = psum.tile([P, STEP_HEADS, HEAD], F32, tag="back")
+            back = psum_back.tile([P, STEP_HEADS, HEAD], F32, tag="back")
             backs[n].append(back)
             for i in range(STEP_HEADS):
                 nc.tensor.transpose(back[:, i, :], biased[n][:, i, P * j : P * (j + 1)], ident[:])

@@ -67,10 +67,13 @@ def tile_fluxjointattention_pa_kernel(
     bias_in = [[baq, bak], [bq, bk]]
     gain_in = [[g_aq, g_ak], [g_q, g_k]]
     stream_tiles = [(0, TEXT_ROWS // P), (TEXT_ROWS // P, ROW_TILES)]
+    stream_rows = [(0, TEXT_ROWS), (TEXT_ROWS, SEQ)]
     outs = [o.rearrange("b s h d -> (b s) (h d)") for o in (out_0, out_1)]
-    text = encoder_hidden_states.flatten_outer_dims()
-    image = hidden_states.flatten_outer_dims()
-    x_groups = [text] + [image[GROUP_ROWS * i : GROUP_ROWS * (i + 1), :] for i in range(GROUPS - 1)]
+    x_in = [encoder_hidden_states.flatten_outer_dims(), hidden_states.flatten_outer_dims()]
+
+    def by_tiles(rows, s):
+        t0, t1 = stream_tiles[s]
+        return rows.rearrange("(p i) w -> p i w", i=t1 - t0)
 
     with ExitStack() as ctx:
         keep = ctx.enter_context(tc.tile_pool(name="keep", bufs=1))
@@ -113,7 +116,8 @@ def tile_fluxjointattention_pa_kernel(
 
         def load_x(g):
             for j in range(GROUP_TILES):
-                nc.sync.dma_start(out=x_rows[g][j][:], in_=x_groups[g][P * j : P * (j + 1), :])
+                s = min(g, 1)
+                nc.sync.dma_start(out=x_rows[g][j][:], in_=by_tiles(x_in[s], s)[:, GROUP_TILES * g + j - stream_tiles[s][0], :])
 
         def load_bias(s):
             for o in range(2):
@@ -152,8 +156,11 @@ def tile_fluxjointattention_pa_kernel(
         load_words(0, 0, 1)
         load_gain(0)
         load_gain(1)
-        nc.sync.dma_start(out=cos[:], in_=rope_cos.rearrange("(t p) d -> p t d", p=P))
-        nc.sync.dma_start(out=sin[:], in_=rope_sin.rearrange("(t p) d -> p t d", p=P))
+        for s in range(2):
+            t0, t1 = stream_tiles[s]
+            r0, r1 = stream_rows[s]
+            nc.sync.dma_start(out=cos[:, t0:t1, :], in_=by_tiles(rope_cos[r0:r1, :], s))
+            nc.sync.dma_start(out=sin[:, t0:t1, :], in_=by_tiles(rope_sin[r0:r1, :], s))
         load_weight(0, 1)
         load_x(1)
         load_bias(1)
@@ -319,8 +326,10 @@ def tile_fluxjointattention_pa_kernel(
                     op=ALU.add,
                 )
                 width = STEP_HEADS * HEAD
+                s = min(g, 1)
+                r0, r1 = stream_rows[s]
                 nc.sync.dma_start(
-                    out=outs[o][P * t : P * (t + 1), width * half : width * (half + 1)],
+                    out=by_tiles(outs[o][r0:r1, width * half : width * (half + 1)], s)[:, t - stream_tiles[s][0], :],
                     in_=result[:].rearrange("p h c e -> p (h c e)"),
                 )
 

@@ -153,6 +153,7 @@ def tile_fluxjointattention_pa_kernel(
         load_scales(0, 0)
         load_words(0, 0, 0)
         load_bias(0)
+        load_x(1)
         load_words(0, 0, 1)
         load_gain(0)
         load_gain(1)
@@ -162,7 +163,6 @@ def tile_fluxjointattention_pa_kernel(
             nc.sync.dma_start(out=cos[:, t0:t1, :], in_=by_tiles(rope_cos[r0:r1, :], s))
             nc.sync.dma_start(out=sin[:, t0:t1, :], in_=by_tiles(rope_sin[r0:r1, :], s))
         load_weight(0, 1)
-        load_x(1)
         load_bias(1)
         load_weight(1, 0)
         load_weight(1, 1)
@@ -203,21 +203,34 @@ def tile_fluxjointattention_pa_kernel(
         x_scales = keep.tile([P, GROUPS, PASSES * GROUP_ROWS], U8, align_bytes=64)
         grouped = {}
 
-        def flip_group(g):
-            grouped[g] = stage.tile([P, PASSES * GROUP_ROWS * PACK], BF16, name="grouped", align_bytes=64)
+        flipped = {}
+
+        def flip_tile(g, j, at_head):
+            words = x_rows[g][j][:].bitcast(F32)
+            if at_head:
+                bank = psum_back.tile([P, PASSES * 2, P], F32, tag="back")
+            else:
+                bank = psum.tile([P, PASSES * 2, P], F32, tag="acc")
+            flipped[g, j] = bank
+            for cu in range(PASSES * 2):
+                first = (K_PASS // 2) * (cu // 2) + cu % 2
+                last = (K_PASS // 2) * (cu // 2 + 1)
+                nc.tensor.transpose(bank[:, cu, :], words[:, first:last:2], ident[:])
+
+        def regroup_tile(g, j):
+            if j == 0:
+                grouped[g] = stage.tile([P, PASSES * GROUP_ROWS * PACK], BF16, name="grouped", align_bytes=64)
             halves = grouped[g][:].bitcast(F32).rearrange("p (c r u) -> p c r u", c=PASSES, u=2)
+            copy = nc.vector.tensor_copy if j % 2 == 0 else nc.scalar.copy
+            copy(
+                out=halves[:, :, P * j : P * (j + 1), :],
+                in_=flipped[g, j][:].rearrange("p (c u) r -> p c r u", u=2),
+            )
+
+        def flip_group(g, at_head=False):
             for j in range(GROUP_TILES):
-                words = x_rows[g][j][:].bitcast(F32)
-                flipped = psum.tile([P, PASSES * 2, P], F32, tag="acc")
-                for cu in range(PASSES * 2):
-                    first = (K_PASS // 2) * (cu // 2) + cu % 2
-                    last = (K_PASS // 2) * (cu // 2 + 1)
-                    nc.tensor.transpose(flipped[:, cu, :], words[:, first:last:2], ident[:])
-                copy = nc.vector.tensor_copy if j % 2 == 0 else nc.scalar.copy
-                copy(
-                    out=halves[:, :, P * j : P * (j + 1), :],
-                    in_=flipped[:].rearrange("p (c u) r -> p c r u", u=2),
-                )
+                flip_tile(g, j, at_head)
+                regroup_tile(g, j)
 
         def quantise_group(g):
             nc.vector.quantize_mx(out=x_codes[:, g, :].bitcast(FP8X4), scales=x_scales[:, g, :], in_=grouped[g][:])
@@ -333,13 +346,18 @@ def tile_fluxjointattention_pa_kernel(
                     in_=result[:].rearrange("p h c e -> p (h c e)"),
                 )
 
-        flip_group(0)
+        flip_group(0, at_head=True)
         bias_columns(0)
+        for j in range(GROUP_TILES):
+            flip_tile(1, j, True)
         quantise_group(0)
+        for j in range(GROUP_TILES):
+            regroup_tile(1, j)
+        quantise_group(1)
         tables(0)
         tables(1)
         for n in range(len(steps) + 2):
-            next_group = n // 4 + 1 if n % 4 == 2 and n // 4 + 1 < GROUPS else None
+            next_group = n // 4 + 1 if n % 4 == 2 and 2 <= n // 4 + 1 < GROUPS else None
             if next_group is not None:
                 flip_group(next_group)
             for part in range(2):
@@ -353,5 +371,5 @@ def tile_fluxjointattention_pa_kernel(
                 rotate(n - 2, n if n < len(steps) and on_vector(n, 1) else None)
             if next_group is not None:
                 quantise_group(next_group)
-            if next_group == 1:
+            if n == 2:
                 bias_columns(1)

@@ -31,6 +31,9 @@ ROW_TILES = SEQ // P
 STEP_HEADS = 4
 BANK_HEADS = 2
 VECTOR_STEP_PERIOD = 4
+TEXT_GROUP = 0
+IMAGE_GROUPS = (1, 2, 3)
+TEXT_PREP_ROUND = 9
 
 FLOPS = 2 * SEQ * MODEL * 2 * MODEL
 
@@ -77,15 +80,13 @@ def tile_fluxjointattention_pa_kernel(
 
     with ExitStack() as ctx:
         keep = ctx.enter_context(tc.tile_pool(name="keep", bufs=1))
-        stage = ctx.enter_context(tc.tile_pool(name="stage", bufs=2))
+        stage = ctx.enter_context(tc.tile_pool(name="stage", bufs=3))
         work = ctx.enter_context(tc.tile_pool(name="work", bufs=6))
         psum = ctx.enter_context(tc.psum_pool(name="psum", bufs=3))
         psum_back = ctx.enter_context(tc.psum_pool(name="psum_back", bufs=5))
         ctx.enter_context(tc.manual_schedule())
 
-        x_rows = [
-            [keep.tile([P, MODEL], BF16, name="x_rows%d%d" % (g, j)) for j in range(GROUP_TILES)] for g in range(GROUPS)
-        ]
+        x_rows = [keep.tile([P, GROUP_TILES, MODEL], BF16, name="x_rows%d" % g) for g in range(GROUPS)]
         w_words = [
             [
                 [
@@ -103,7 +104,7 @@ def tile_fluxjointattention_pa_kernel(
         gain = [[keep.tile([P, HEAD], BF16, name="gain%d%d" % (s, o)) for o in range(2)] for s in range(2)]
         cos = keep.tile([P, ROW_TILES, HEAD], BF16)
         sin = keep.tile([P, ROW_TILES, HEAD], BF16)
-        for s in range(2):
+        for s in (1, 0):
             nc.vector.memset(bias_rows[s][:], 0.0)
             for o in range(2):
                 nc.vector.memset(w_planes[s][o][:].bitcast(I32), 0)
@@ -114,10 +115,12 @@ def tile_fluxjointattention_pa_kernel(
         table_warmer = keep.tile([P, 1], F32)
         nc.scalar.activation(out=table_warmer[:], in_=eps[:], func=ACT.Abs_reciprocal_sqrt)
 
-        def load_x(g):
-            for j in range(GROUP_TILES):
-                s = min(g, 1)
-                nc.sync.dma_start(out=x_rows[g][j][:], in_=by_tiles(x_in[s], s)[:, GROUP_TILES * g + j - stream_tiles[s][0], :])
+        def load_x(g, pieces):
+            s = min(g, 1)
+            first = GROUP_TILES * g - stream_tiles[s][0]
+            size = GROUP_TILES // pieces
+            for j in range(0, GROUP_TILES, size):
+                nc.sync.dma_start(out=x_rows[g][:, j : j + size, :], in_=by_tiles(x_in[s], s)[:, first + j : first + j + size, :])
 
         def load_bias(s):
             for o in range(2):
@@ -125,9 +128,14 @@ def tile_fluxjointattention_pa_kernel(
                     out=bias_rows[s][HEADS * o : HEADS * (o + 1), :], in_=bias_in[s][o].rearrange("(h d) -> h d", d=HEAD)
                 )
 
-        def load_gain(s):
-            for o in range(2):
-                nc.sync.dma_start(out=gain[s][o][:], in_=gain_in[s][o].partition_broadcast(P))
+        def load_gain(s, o):
+            nc.sync.dma_start(out=gain[s][o][:], in_=gain_in[s][o].partition_broadcast(P))
+
+        def load_rope(s):
+            t0, t1 = stream_tiles[s]
+            r0, r1 = stream_rows[s]
+            nc.sync.dma_start(out=cos[:, t0:t1, :], in_=by_tiles(rope_cos[r0:r1, :], s))
+            nc.sync.dma_start(out=sin[:, t0:t1, :], in_=by_tiles(rope_sin[r0:r1, :], s))
 
         def load_scales(s, o):
             for quad in range(4):
@@ -144,30 +152,29 @@ def tile_fluxjointattention_pa_kernel(
                 in_=words_in[s][o].rearrange("g p n t -> p g (n t)")[:, :, width * half : width * (half + 1)].bitcast(I32),
             )
 
-        def load_weight(s, o):
-            load_scales(s, o)
-            for half in range(HEADS // STEP_HEADS):
-                load_words(s, o, half)
-
-        load_x(0)
-        load_scales(0, 0)
-        load_words(0, 0, 0)
-        load_bias(0)
-        load_x(1)
-        load_words(0, 0, 1)
-        load_gain(0)
-        load_gain(1)
-        for s in range(2):
-            t0, t1 = stream_tiles[s]
-            r0, r1 = stream_rows[s]
-            nc.sync.dma_start(out=cos[:, t0:t1, :], in_=by_tiles(rope_cos[r0:r1, :], s))
-            nc.sync.dma_start(out=sin[:, t0:t1, :], in_=by_tiles(rope_sin[r0:r1, :], s))
-        load_weight(0, 1)
+        load_x(1, GROUP_TILES)
         load_bias(1)
-        load_weight(1, 0)
-        load_weight(1, 1)
-        load_x(2)
-        load_x(3)
+        load_x(2, 1)
+        load_x(3, 1)
+        load_scales(1, 0)
+        load_words(1, 0, 0)
+        load_words(1, 0, 1)
+        load_gain(1, 0)
+        load_rope(1)
+        load_gain(1, 1)
+        load_rope(0)
+        load_gain(0, 0)
+        load_gain(0, 1)
+        load_scales(1, 1)
+        load_scales(0, 0)
+        load_scales(0, 1)
+        load_words(1, 1, 0)
+        load_words(1, 1, 1)
+        load_x(0, 1)
+        load_bias(0)
+        for o in range(2):
+            for half in range(HEADS // STEP_HEADS):
+                load_words(0, o, half)
 
         bias_col = [keep.tile([P, 2 * HEADS], F32, name="bias_col%d" % s) for s in range(2)]
         table = [keep.tile([P, ROW_TILES, 2, HEAD], F32, name="table%d" % o) for o in range(2)]
@@ -206,7 +213,7 @@ def tile_fluxjointattention_pa_kernel(
         flipped = {}
 
         def flip_tile(g, j, at_head):
-            words = x_rows[g][j][:].bitcast(F32)
+            words = x_rows[g][:, j, :].bitcast(F32)
             if at_head:
                 bank = psum_back.tile([P, PASSES * 2, P], F32, tag="back")
             else:
@@ -235,7 +242,9 @@ def tile_fluxjointattention_pa_kernel(
         def quantise_group(g):
             nc.vector.quantize_mx(out=x_codes[:, g, :].bitcast(FP8X4), scales=x_scales[:, g, :], in_=grouped[g][:])
 
-        steps = [(g, o, half) for g in range(GROUPS) for o in range(2) for half in range(HEADS // STEP_HEADS)]
+        halves_of_heads = range(HEADS // STEP_HEADS)
+        steps = [(g, o, half) for o in range(2) for g in IMAGE_GROUPS for half in halves_of_heads]
+        steps += [(TEXT_GROUP, o, half) for o in range(2) for half in halves_of_heads]
         accs = {}
         biased = {}
         backs = {}
@@ -346,20 +355,22 @@ def tile_fluxjointattention_pa_kernel(
                     in_=result[:].rearrange("p h c e -> p (h c e)"),
                 )
 
-        flip_group(0, at_head=True)
-        bias_columns(0)
-        for j in range(GROUP_TILES):
-            flip_tile(1, j, True)
-        quantise_group(0)
-        for j in range(GROUP_TILES):
-            regroup_tile(1, j)
+        flip_group(1, at_head=True)
+        bias_columns(1)
+        for g in (2, 3):
+            for j in range(GROUP_TILES):
+                flip_tile(g, j, True)
         quantise_group(1)
-        tables(0)
+        for g in (2, 3):
+            for j in range(GROUP_TILES):
+                regroup_tile(g, j)
+        quantise_group(2)
+        quantise_group(3)
         tables(1)
+        tables(0)
         for n in range(len(steps) + 2):
-            next_group = n // 4 + 1 if n % 4 == 2 and 2 <= n // 4 + 1 < GROUPS else None
-            if next_group is not None:
-                flip_group(next_group)
+            if n == TEXT_PREP_ROUND:
+                flip_group(TEXT_GROUP)
             for part in range(2):
                 if n < len(steps):
                     project(n, part)
@@ -369,7 +380,6 @@ def tile_fluxjointattention_pa_kernel(
                 root(n - 1)
             if n >= 2:
                 rotate(n - 2, n if n < len(steps) and on_vector(n, 1) else None)
-            if next_group is not None:
-                quantise_group(next_group)
-            if n == 2:
-                bias_columns(1)
+            if n == TEXT_PREP_ROUND:
+                quantise_group(TEXT_GROUP)
+                bias_columns(0)

@@ -30,7 +30,8 @@ GROUP_TILES = GROUP_ROWS // P
 ROW_TILES = SEQ // P
 STEP_HEADS = 4
 BANK_HEADS = 2
-VECTOR_STEP_PERIOD = 4
+VECTOR_STEPS = (2, 4, 6, 8, 10, 12, 14)
+LAST_PIECES = 2
 TEXT_GROUP = 0
 IMAGE_GROUPS = (1, 2, 3)
 TEXT_PREP_ROUND = 9
@@ -278,7 +279,7 @@ def tile_fluxjointattention_pa_kernel(
                 add_bias(n, b)
 
         def on_vector(n, b):
-            return b == 1 and n % VECTOR_STEP_PERIOD == VECTOR_STEP_PERIOD - 1
+            return b == 1 and n in VECTOR_STEPS
 
         def add_bias(n, b):
             g, o, half = steps[n]
@@ -323,37 +324,41 @@ def tile_fluxjointattention_pa_kernel(
 
         def rotate(n, between):
             g, o, half = steps[n]
+            s = min(g, 1)
+            r0, r1 = stream_rows[s]
             for j in range(GROUP_TILES):
                 if j == 1 and between is not None:
                     add_bias(between, 1)
                 t = GROUP_TILES * g + j
                 back = backs[n][j]
+                last = (n, j) == (len(steps) - 1, GROUP_TILES - 1)
+                piece_heads = STEP_HEADS // LAST_PIECES if last else STEP_HEADS
                 products = work.tile([P, STEP_HEADS, 2, HEAD], F32, name="products")
-                for i in range(STEP_HEADS):
-                    r = inv_rms[n][:, STEP_HEADS * j + i : STEP_HEADS * j + i + 1]
-                    nc.vector.scalar_tensor_tensor(
-                        out=products[:, i, :, :],
-                        in0=back[:, i, :].unsqueeze(1).to_broadcast([P, 2, HEAD]),
-                        scalar=r,
-                        in1=table[o][:, t, :, :],
-                        op0=ALU.mult,
-                        op1=ALU.mult,
-                    )
                 result = work.tile([P, STEP_HEADS, PAIRS, 2], F32, name="result")
-                adder = nc.vector if (n, j) == (len(steps) - 1, GROUP_TILES - 1) else nc.gpsimd
-                adder.tensor_tensor(
-                    out=result[:],
-                    in0=products[:, :, 0, :].rearrange("p h (c e) -> p h c e", e=2),
-                    in1=products[:, :, 1, :].rearrange("p h (c e) -> p h c e", e=2)[:, :, :, ::-1],
-                    op=ALU.add,
-                )
-                width = STEP_HEADS * HEAD
-                s = min(g, 1)
-                r0, r1 = stream_rows[s]
-                nc.sync.dma_start(
-                    out=by_tiles(outs[o][r0:r1, width * half : width * (half + 1)], s)[:, t - stream_tiles[s][0], :],
-                    in_=result[:].rearrange("p h c e -> p (h c e)"),
-                )
+                for i0 in range(0, STEP_HEADS, piece_heads):
+                    heads = slice(i0, i0 + piece_heads)
+                    for i in range(i0, i0 + piece_heads):
+                        r = inv_rms[n][:, STEP_HEADS * j + i : STEP_HEADS * j + i + 1]
+                        nc.vector.scalar_tensor_tensor(
+                            out=products[:, i, :, :],
+                            in0=back[:, i, :].unsqueeze(1).to_broadcast([P, 2, HEAD]),
+                            scalar=r,
+                            in1=table[o][:, t, :, :],
+                            op0=ALU.mult,
+                            op1=ALU.mult,
+                        )
+                    adder = nc.vector if last else nc.gpsimd
+                    adder.tensor_tensor(
+                        out=result[:, heads, :, :],
+                        in0=products[:, heads, 0, :].rearrange("p h (c e) -> p h c e", e=2),
+                        in1=products[:, heads, 1, :].rearrange("p h (c e) -> p h c e", e=2)[:, :, :, ::-1],
+                        op=ALU.add,
+                    )
+                    first = HEAD * (STEP_HEADS * half + i0)
+                    nc.sync.dma_start(
+                        out=by_tiles(outs[o][r0:r1, first : first + HEAD * piece_heads], s)[:, t - stream_tiles[s][0], :],
+                        in_=result[:, heads, :, :].rearrange("p h c e -> p (h c e)"),
+                    )
 
         flip_group(1, at_head=True)
         bias_columns(1)

@@ -30,8 +30,9 @@ GROUP_TILES = GROUP_ROWS // P
 ROW_TILES = SEQ // P
 STEP_HEADS = 4
 BANK_HEADS = 2
-VECTOR_STEPS = (2, 4, 6, 8, 10, 12, 14)
+VECTOR_STEPS = (4, 6, 8, 10, 12, 14)
 LAST_PIECES = 2
+LAST_IMAGE_PREP_ROUND = 2
 TEXT_GROUP = 0
 IMAGE_GROUPS = (1, 2, 3)
 TEXT_PREP_ROUND = 9
@@ -156,12 +157,12 @@ def tile_fluxjointattention_pa_kernel(
         load_x(1, GROUP_TILES)
         load_bias(1)
         load_x(2, 1)
-        load_x(3, 1)
         load_scales(1, 0)
         load_words(1, 0, 0)
         load_words(1, 0, 1)
         load_gain(1, 0)
         load_rope(1)
+        load_x(3, 1)
         load_gain(1, 1)
         load_rope(0)
         load_gain(0, 0)
@@ -186,6 +187,18 @@ def tile_fluxjointattention_pa_kernel(
             bias_ps = psum.tile([P, P], F32, tag="acc")
             nc.tensor.transpose(bias_ps[:], bias_rows32[:], ident[:])
             nc.vector.tensor_copy(out=bias_col[s][:], in_=bias_ps[:, 0 : 2 * HEADS])
+
+        late_bias = {}
+
+        def widen_late_bias(s):
+            rows32 = keep.tile([P, P], F32, name="late_bias_rows32")
+            late_bias["rows32"] = rows32
+            nc.scalar.copy(out=rows32[:], in_=bias_rows[s][:])
+
+        def flip_late_bias(s):
+            bias_ps = psum.tile([P, P], F32, tag="acc")
+            nc.tensor.transpose(bias_ps[:], late_bias["rows32"][:], ident[:])
+            nc.scalar.copy(out=bias_col[s][:], in_=bias_ps[:, 0 : 2 * HEADS])
 
         def tables(s):
             t0, t1 = stream_tiles[s]
@@ -229,7 +242,7 @@ def tile_fluxjointattention_pa_kernel(
             if j == 0:
                 grouped[g] = stage.tile([P, PASSES * GROUP_ROWS * PACK], BF16, name="grouped", align_bytes=64)
             halves = grouped[g][:].bitcast(F32).rearrange("p (c r u) -> p c r u", c=PASSES, u=2)
-            copy = nc.vector.tensor_copy if j % 2 == 0 else nc.scalar.copy
+            copy = nc.vector.tensor_copy if j == 0 and g in IMAGE_GROUPS[0:2] else nc.scalar.copy
             copy(
                 out=halves[:, :, P * j : P * (j + 1), :],
                 in_=flipped[g, j][:].rearrange("p (c u) r -> p c r u", u=2),
@@ -362,20 +375,23 @@ def tile_fluxjointattention_pa_kernel(
 
         flip_group(1, at_head=True)
         bias_columns(1)
-        for g in (2, 3):
-            for j in range(GROUP_TILES):
-                flip_tile(g, j, True)
+        for j in range(GROUP_TILES):
+            flip_tile(2, j, True)
         quantise_group(1)
-        for g in (2, 3):
-            for j in range(GROUP_TILES):
-                regroup_tile(g, j)
+        for j in range(GROUP_TILES):
+            regroup_tile(2, j)
         quantise_group(2)
-        quantise_group(3)
         tables(1)
         tables(0)
         for n in range(len(steps) + 2):
+            if n == TEXT_PREP_ROUND - 1:
+                widen_late_bias(0)
             if n == TEXT_PREP_ROUND:
                 flip_group(TEXT_GROUP)
+            if n == TEXT_PREP_ROUND + 1:
+                flip_late_bias(0)
+            if n == LAST_IMAGE_PREP_ROUND:
+                flip_group(3)
             for part in range(2):
                 if n < len(steps):
                     project(n, part)
@@ -385,6 +401,7 @@ def tile_fluxjointattention_pa_kernel(
                 root(n - 1)
             if n >= 2:
                 rotate(n - 2, n if n < len(steps) and on_vector(n, 1) else None)
+            if n == LAST_IMAGE_PREP_ROUND:
+                quantise_group(3)
             if n == TEXT_PREP_ROUND:
                 quantise_group(TEXT_GROUP)
-                bias_columns(0)

@@ -31,6 +31,7 @@ ROW_TILES = SEQ // P
 STEP_HEADS = 4
 BANK_HEADS = 2
 VECTOR_STEPS = (4, 6, 8, 10, 12, 14)
+MERGED_STEPS = 12
 LAST_PIECES = 2
 LAST_IMAGE_PREP_ROUND = 2
 TEXT_GROUP = 0
@@ -339,39 +340,46 @@ def tile_fluxjointattention_pa_kernel(
             g, o, half = steps[n]
             s = min(g, 1)
             r0, r1 = stream_rows[s]
+            merged = n < MERGED_STEPS
+            products = work.tile([P, GROUP_TILES * STEP_HEADS, 2, HEAD], F32, name="products")
+            result = work.tile([P, GROUP_TILES * STEP_HEADS, PAIRS, 2], F32, name="result")
             for j in range(GROUP_TILES):
                 if j == 1 and between is not None:
                     add_bias(between, 1)
                 t = GROUP_TILES * g + j
                 back = backs[n][j]
                 last = (n, j) == (len(steps) - 1, GROUP_TILES - 1)
+                on_vector_add = n == len(steps) - 1
                 piece_heads = STEP_HEADS // LAST_PIECES if last else STEP_HEADS
-                products = work.tile([P, STEP_HEADS, 2, HEAD], F32, name="products")
-                result = work.tile([P, STEP_HEADS, PAIRS, 2], F32, name="result")
                 for i0 in range(0, STEP_HEADS, piece_heads):
-                    heads = slice(i0, i0 + piece_heads)
                     for i in range(i0, i0 + piece_heads):
                         r = inv_rms[n][:, STEP_HEADS * j + i : STEP_HEADS * j + i + 1]
                         nc.vector.scalar_tensor_tensor(
-                            out=products[:, i, :, :],
+                            out=products[:, STEP_HEADS * j + i, :, :],
                             in0=back[:, i, :].unsqueeze(1).to_broadcast([P, 2, HEAD]),
                             scalar=r,
                             in1=table[o][:, t, :, :],
                             op0=ALU.mult,
                             op1=ALU.mult,
                         )
-                    adder = nc.vector if last else nc.gpsimd
+                    if merged and j == 0:
+                        continue
+                    first_block = 0 if merged else STEP_HEADS * j + i0
+                    blocks = slice(first_block, STEP_HEADS * j + i0 + piece_heads)
+                    adder = nc.vector if on_vector_add else nc.gpsimd
                     adder.tensor_tensor(
-                        out=result[:, heads, :, :],
-                        in0=products[:, heads, 0, :].rearrange("p h (c e) -> p h c e", e=2),
-                        in1=products[:, heads, 1, :].rearrange("p h (c e) -> p h c e", e=2)[:, :, :, ::-1],
+                        out=result[:, blocks, :, :],
+                        in0=products[:, blocks, 0, :].rearrange("p h (c e) -> p h c e", e=2),
+                        in1=products[:, blocks, 1, :].rearrange("p h (c e) -> p h c e", e=2)[:, :, :, ::-1],
                         op=ALU.add,
                     )
-                    first = HEAD * (STEP_HEADS * half + i0)
-                    nc.sync.dma_start(
-                        out=by_tiles(outs[o][r0:r1, first : first + HEAD * piece_heads], s)[:, t - stream_tiles[s][0], :],
-                        in_=result[:, heads, :, :].rearrange("p h c e -> p (h c e)"),
-                    )
+                    for b0 in range(first_block, blocks.stop, piece_heads):
+                        first = HEAD * (STEP_HEADS * half + b0 % STEP_HEADS)
+                        tile_of_stream = GROUP_TILES * g + b0 // STEP_HEADS - stream_tiles[s][0]
+                        nc.sync.dma_start(
+                            out=by_tiles(outs[o][r0:r1, first : first + HEAD * piece_heads], s)[:, tile_of_stream, :],
+                            in_=result[:, b0 : b0 + piece_heads, :, :].rearrange("p h c e -> p (h c e)"),
+                        )
 
         flip_group(1, at_head=True)
         bias_columns(1)

@@ -30,7 +30,7 @@ GROUP_TILES = GROUP_ROWS // P
 ROW_TILES = SEQ // P
 STEP_HEADS = 4
 BANK_HEADS = 2
-VECTOR_STEPS = (4, 6, 8, 10, 12, 14)
+VECTOR_STEPS = (1, 3, 4, 6, 7, 8, 10, 12, 14)
 MERGED_STEPS = 12
 LAST_PIECES = 2
 LAST_IMAGE_PREP_ROUND = 2
@@ -201,25 +201,29 @@ def tile_fluxjointattention_pa_kernel(
             nc.tensor.transpose(bias_ps[:], late_bias["rows32"][:], ident[:])
             nc.scalar.copy(out=bias_col[s][:], in_=bias_ps[:, 0 : 2 * HEADS])
 
-        def tables(s):
+        def cos_table(s, o):
             t0, t1 = stream_tiles[s]
-            for o in range(2):
-                nc.gpsimd.tensor_tensor(
-                    out=table[o][:, t0:t1, 0, :],
-                    in0=cos[:, t0:t1, :],
-                    in1=gain[s][o][:].unsqueeze(1).to_broadcast([P, t1 - t0, HEAD]),
-                    op=ALU.mult,
-                )
-                gain_pairs = gain[s][o][:].rearrange("p (c e) -> p c e", e=2)
-                signed = keep.tile([P, PAIRS, 2], F32, name="signed%d%d" % (s, o))
-                nc.vector.tensor_copy(out=signed[:, :, 0], in_=gain_pairs[:, :, 0])
-                nc.vector.tensor_scalar_mul(out=signed[:, :, 1], in0=gain_pairs[:, :, 1], scalar1=-1.0)
-                nc.vector.tensor_tensor(
-                    out=table[o][:, t0:t1, 1, :].rearrange("p t (c e) -> p t c e", e=2),
-                    in0=sin[:, t0:t1, :].rearrange("p t (c e) -> p t c e", e=2)[:, :, :, ::-1],
-                    in1=signed[:].unsqueeze(1).to_broadcast([P, t1 - t0, PAIRS, 2]),
-                    op=ALU.mult,
-                )
+            nc.gpsimd.tensor_tensor(
+                out=table[o][:, t0:t1, 0, :],
+                in0=cos[:, t0:t1, :],
+                in1=gain[s][o][:].unsqueeze(1).to_broadcast([P, t1 - t0, HEAD]),
+                op=ALU.mult,
+            )
+
+        def sin_table(s, o, engine):
+            t0, t1 = stream_tiles[s]
+            gain_pairs = gain[s][o][:].rearrange("p (c e) -> p c e", e=2)
+            signed = keep.tile([P, PAIRS, 2], F32, name="signed%d%d" % (s, o))
+            engine.tensor_copy(out=signed[:, :, 0], in_=gain_pairs[:, :, 0])
+            engine.tensor_scalar(
+                out=signed[:, :, 1], in0=gain_pairs[:, :, 1], scalar1=-1.0, scalar2=0.0, op0=ALU.mult, op1=ALU.add
+            )
+            engine.tensor_tensor(
+                out=table[o][:, t0:t1, 1, :].rearrange("p t (c e) -> p t c e", e=2),
+                in0=sin[:, t0:t1, :].rearrange("p t (c e) -> p t c e", e=2)[:, :, :, ::-1],
+                in1=signed[:].unsqueeze(1).to_broadcast([P, t1 - t0, PAIRS, 2]),
+                op=ALU.mult,
+            )
 
         x_codes = keep.tile([P, GROUPS, PASSES * GROUP_ROWS], U32, align_bytes=64)
         x_scales = keep.tile([P, GROUPS, PASSES * GROUP_ROWS], U8, align_bytes=64)
@@ -389,8 +393,12 @@ def tile_fluxjointattention_pa_kernel(
         for j in range(GROUP_TILES):
             regroup_tile(2, j)
         quantise_group(2)
-        tables(1)
-        tables(0)
+        cos_table(1, 0)
+        sin_table(1, 0, nc.vector)
+        cos_table(1, 1)
+        sin_table(1, 1, nc.gpsimd)
+        for o in range(2):
+            cos_table(0, o)
         for n in range(len(steps) + 2):
             if n == TEXT_PREP_ROUND - 1:
                 widen_late_bias(0)
@@ -409,6 +417,11 @@ def tile_fluxjointattention_pa_kernel(
                 root(n - 1)
             if n >= 2:
                 rotate(n - 2, n if n < len(steps) and on_vector(n, 1) else None)
+            elif on_vector(n, 1):
+                add_bias(n, 1)
+            if n == 1:
+                for o in range(2):
+                    sin_table(0, o, nc.vector)
             if n == LAST_IMAGE_PREP_ROUND:
                 quantise_group(3)
             if n == TEXT_PREP_ROUND:

from contextlib import ExitStack

import concourse.mybir as mybir
from concourse.masks import make_identity

F32 = mybir.dt.float32
BF16 = mybir.dt.bfloat16
I32 = mybir.dt.int32
U32 = mybir.dt.uint32
U8 = mybir.dt.uint8
FP8X4 = mybir.dt.float8_e4m3fn_x4
ACT = mybir.ActivationFunctionType
ALU = mybir.AluOpType

P = 128
PACK = 4
K_PASS = P * PACK
MODEL = 1024
PASSES = MODEL // K_PASS
HEAD = 128
HEADS = MODEL // HEAD
PAIRS = HEAD // 2
EPS = 1e-6

TEXT_ROWS = 256
SEQ = 1024
GROUP_ROWS = 256
GROUPS = SEQ // GROUP_ROWS
GROUP_TILES = GROUP_ROWS // P
ROW_TILES = SEQ // P
STEP_HEADS = 4
BANK_HEADS = 2
VECTOR_STEPS = (1, 3, 4, 6, 7, 8, 10, 12, 14)
MERGED_STEPS = 12
LAST_PIECES = 2
LAST_IMAGE_PREP_ROUND = 2
TEXT_GROUP = 0
IMAGE_GROUPS = (1, 2, 3)
TEXT_PREP_ROUND = 9

FLOPS = 2 * SEQ * MODEL * 2 * MODEL


def tile_fluxjointattention_pa_kernel(
    tc,
    hidden_states,
    encoder_hidden_states,
    rope_cos,
    rope_sin,
    Wq_words,
    Wq_scales,
    Wk_words,
    Wk_scales,
    Waq_words,
    Waq_scales,
    Wak_words,
    Wak_scales,
    bq,
    bk,
    baq,
    bak,
    g_q,
    g_k,
    g_aq,
    g_ak,
    out_0,
    out_1,
):
    nc = tc.nc

    words_in = [[Waq_words, Wak_words], [Wq_words, Wk_words]]
    scales_in = [[Waq_scales, Wak_scales], [Wq_scales, Wk_scales]]
    bias_in = [[baq, bak], [bq, bk]]
    gain_in = [[g_aq, g_ak], [g_q, g_k]]
    stream_tiles = [(0, TEXT_ROWS // P), (TEXT_ROWS // P, ROW_TILES)]
    stream_rows = [(0, TEXT_ROWS), (TEXT_ROWS, SEQ)]
    outs = [o.rearrange("b s h d -> (b s) (h d)") for o in (out_0, out_1)]
    x_in = [encoder_hidden_states.flatten_outer_dims(), hidden_states.flatten_outer_dims()]

    def by_tiles(rows, s):
        t0, t1 = stream_tiles[s]
        return rows.rearrange("(p i) w -> p i w", i=t1 - t0)

    with ExitStack() as ctx:
        keep = ctx.enter_context(tc.tile_pool(name="keep", bufs=1))
        stage = ctx.enter_context(tc.tile_pool(name="stage", bufs=3))
        work = ctx.enter_context(tc.tile_pool(name="work", bufs=6))
        psum = ctx.enter_context(tc.psum_pool(name="psum", bufs=3))
        psum_back = ctx.enter_context(tc.psum_pool(name="psum_back", bufs=5))
        ctx.enter_context(tc.manual_schedule())

        x_rows = [keep.tile([P, GROUP_TILES, MODEL], BF16, name="x_rows%d" % g) for g in range(GROUPS)]
        w_words = [
            [
                [
                    keep.tile([P, PASSES, STEP_HEADS * HEAD], U32, name="w_words%d%d%d" % (s, o, half), align_bytes=64)
                    for half in range(HEADS // STEP_HEADS)
                ]
                for o in range(2)
            ]
            for s in range(2)
        ]
        w_planes = [
            [keep.tile([P, MODEL], U8, name="w_planes%d%d" % (s, o), align_bytes=64) for o in range(2)] for s in range(2)
        ]
        bias_rows = [keep.tile([P, P], BF16, name="bias_rows%d" % s) for s in range(2)]
        gain = [[keep.tile([P, HEAD], BF16, name="gain%d%d" % (s, o)) for o in range(2)] for s in range(2)]
        cos = keep.tile([P, ROW_TILES, HEAD], BF16)
        sin = keep.tile([P, ROW_TILES, HEAD], BF16)
        for s in (1, 0):
            nc.vector.memset(bias_rows[s][:], 0.0)
            for o in range(2):
                nc.vector.memset(w_planes[s][o][:].bitcast(I32), 0)
        eps = keep.tile([P, 1], F32)
        nc.vector.memset(eps[:], EPS)
        ident = keep.tile([P, P], F32)
        make_identity(nc, ident[:])
        table_warmer = keep.tile([P, 1], F32)
        nc.scalar.activation(out=table_warmer[:], in_=eps[:], func=ACT.Abs_reciprocal_sqrt)

        def load_x(g, pieces):
            s = min(g, 1)
            first = GROUP_TILES * g - stream_tiles[s][0]
            size = GROUP_TILES // pieces
            for j in range(0, GROUP_TILES, size):
                nc.sync.dma_start(out=x_rows[g][:, j : j + size, :], in_=by_tiles(x_in[s], s)[:, first + j : first + j + size, :])

        def load_bias(s):
            for o in range(2):
                nc.sync.dma_start(
                    out=bias_rows[s][HEADS * o : HEADS * (o + 1), :], in_=bias_in[s][o].rearrange("(h d) -> h d", d=HEAD)
                )

        def load_gain(s, o):
            nc.sync.dma_start(out=gain[s][o][:], in_=gain_in[s][o].partition_broadcast(P))

        def load_rope(s):
            t0, t1 = stream_tiles[s]
            r0, r1 = stream_rows[s]
            nc.sync.dma_start(out=cos[:, t0:t1, :], in_=by_tiles(rope_cos[r0:r1, :], s))
            nc.sync.dma_start(out=sin[:, t0:t1, :], in_=by_tiles(rope_sin[r0:r1, :], s))

        def load_scales(s, o):
            for quad in range(4):
                first = 32 * quad
                nc.sync.dma_start(
                    out=w_planes[s][o][first : first + 2 * PACK, :].bitcast(I32),
                    in_=scales_in[s][o][:, 4 * quad : 4 * quad + 4, :].bitcast(I32),
                )

        def load_words(s, o, half):
            width = STEP_HEADS * HEAD * PACK
            nc.sync.dma_start(
                out=w_words[s][o][half][:].bitcast(I32),
                in_=words_in[s][o].rearrange("g p n t -> p g (n t)")[:, :, width * half : width * (half + 1)].bitcast(I32),
            )

        load_x(1, GROUP_TILES)
        load_bias(1)
        load_x(2, 1)
        load_scales(1, 0)
        load_words(1, 0, 0)
        load_words(1, 0, 1)
        load_gain(1, 0)
        load_rope(1)
        load_x(3, 1)
        load_gain(1, 1)
        load_rope(0)
        load_gain(0, 0)
        load_gain(0, 1)
        load_scales(1, 1)
        load_scales(0, 0)
        load_scales(0, 1)
        load_words(1, 1, 0)
        load_words(1, 1, 1)
        load_x(0, 1)
        load_bias(0)
        for o in range(2):
            for half in range(HEADS // STEP_HEADS):
                load_words(0, o, half)

        bias_col = [keep.tile([P, 2 * HEADS], F32, name="bias_col%d" % s) for s in range(2)]
        table = [keep.tile([P, ROW_TILES, 2, HEAD], F32, name="table%d" % o) for o in range(2)]

        def bias_columns(s):
            bias_rows32 = keep.tile([P, P], F32, name="bias_rows32_%d" % s)
            nc.vector.tensor_copy(out=bias_rows32[:], in_=bias_rows[s][:])
            bias_ps = psum.tile([P, P], F32, tag="acc")
            nc.tensor.transpose(bias_ps[:], bias_rows32[:], ident[:])
            nc.vector.tensor_copy(out=bias_col[s][:], in_=bias_ps[:, 0 : 2 * HEADS])

        late_bias = {}

        def widen_late_bias(s):
            rows32 = keep.tile([P, P], F32, name="late_bias_rows32")
            late_bias["rows32"] = rows32
            nc.scalar.copy(out=rows32[:], in_=bias_rows[s][:])

        def flip_late_bias(s):
            bias_ps = psum.tile([P, P], F32, tag="acc")
            nc.tensor.transpose(bias_ps[:], late_bias["rows32"][:], ident[:])
            nc.scalar.copy(out=bias_col[s][:], in_=bias_ps[:, 0 : 2 * HEADS])

        def cos_table(s, o):
            t0, t1 = stream_tiles[s]
            nc.gpsimd.tensor_tensor(
                out=table[o][:, t0:t1, 0, :],
                in0=cos[:, t0:t1, :],
                in1=gain[s][o][:].unsqueeze(1).to_broadcast([P, t1 - t0, HEAD]),
                op=ALU.mult,
            )

        def sin_table(s, o, engine):
            t0, t1 = stream_tiles[s]
            gain_pairs = gain[s][o][:].rearrange("p (c e) -> p c e", e=2)
            signed = keep.tile([P, PAIRS, 2], F32, name="signed%d%d" % (s, o))
            engine.tensor_copy(out=signed[:, :, 0], in_=gain_pairs[:, :, 0])
            engine.tensor_scalar(
                out=signed[:, :, 1], in0=gain_pairs[:, :, 1], scalar1=-1.0, scalar2=0.0, op0=ALU.mult, op1=ALU.add
            )
            engine.tensor_tensor(
                out=table[o][:, t0:t1, 1, :].rearrange("p t (c e) -> p t c e", e=2),
                in0=sin[:, t0:t1, :].rearrange("p t (c e) -> p t c e", e=2)[:, :, :, ::-1],
                in1=signed[:].unsqueeze(1).to_broadcast([P, t1 - t0, PAIRS, 2]),
                op=ALU.mult,
            )

        x_codes = keep.tile([P, GROUPS, PASSES * GROUP_ROWS], U32, align_bytes=64)
        x_scales = keep.tile([P, GROUPS, PASSES * GROUP_ROWS], U8, align_bytes=64)
        grouped = {}

        flipped = {}

        def flip_tile(g, j, at_head):
            words = x_rows[g][:, j, :].bitcast(F32)
            if at_head:
                bank = psum_back.tile([P, PASSES * 2, P], F32, tag="back")
            else:
                bank = psum.tile([P, PASSES * 2, P], F32, tag="acc")
            flipped[g, j] = bank
            for cu in range(PASSES * 2):
                first = (K_PASS // 2) * (cu // 2) + cu % 2
                last = (K_PASS // 2) * (cu // 2 + 1)
                nc.tensor.transpose(bank[:, cu, :], words[:, first:last:2], ident[:])

        def regroup_tile(g, j):
            if j == 0:
                grouped[g] = stage.tile([P, PASSES * GROUP_ROWS * PACK], BF16, name="grouped", align_bytes=64)
            halves = grouped[g][:].bitcast(F32).rearrange("p (c r u) -> p c r u", c=PASSES, u=2)
            copy = nc.vector.tensor_copy if j == 0 and g in IMAGE_GROUPS[0:2] else nc.scalar.copy
            copy(
                out=halves[:, :, P * j : P * (j + 1), :],
                in_=flipped[g, j][:].rearrange("p (c u) r -> p c r u", u=2),
            )

        def flip_group(g, at_head=False):
            for j in range(GROUP_TILES):
                flip_tile(g, j, at_head)
                regroup_tile(g, j)

        def quantise_group(g):
            nc.vector.quantize_mx(out=x_codes[:, g, :].bitcast(FP8X4), scales=x_scales[:, g, :], in_=grouped[g][:])

        halves_of_heads = range(HEADS // STEP_HEADS)
        steps = [(g, o, half) for o in range(2) for g in IMAGE_GROUPS for half in halves_of_heads]
        steps += [(TEXT_GROUP, o, half) for o in range(2) for half in halves_of_heads]
        accs = {}
        biased = {}
        backs = {}
        sumsq = {}
        rms = {}
        inv_rms = {}

        def project(n, b):
            g, o, half = steps[n]
            s = min(g, 1)
            if b == 0:
                biased[n] = work.tile([P, STEP_HEADS, GROUP_ROWS], F32, name="biased")
            acc = psum.tile([P, BANK_HEADS, GROUP_ROWS], F32, tag="acc")
            accs[n, b] = acc
            for i in range(BANK_HEADS):
                h = STEP_HEADS * half + BANK_HEADS * b + i
                cols = slice(HEAD * h, HEAD * (h + 1))
                own_cols = slice(HEAD * (BANK_HEADS * b + i), HEAD * (BANK_HEADS * b + i + 1))
                for c in range(PASSES):
                    rows = slice(GROUP_ROWS * c, GROUP_ROWS * (c + 1))
                    nc.tensor.matmul_mx(
                        out=acc[:, i, :],
                        lhsT=w_words[s][o][half][:, c, own_cols].bitcast(FP8X4),
                        lhsT_scale=w_planes[s][o][4 * c : P, cols],
                        rhs=x_codes[:, g, rows].bitcast(FP8X4),
                        rhs_scale=x_scales[:, g, rows],
                        start=(c == 0),
                        stop=(c == PASSES - 1),
                    )
            if not on_vector(n, b):
                add_bias(n, b)

        def on_vector(n, b):
            return b == 1 and n in VECTOR_STEPS

        def add_bias(n, b):
            g, o, half = steps[n]
            s = min(g, 1)
            for i in range(BANK_HEADS):
                col = HEADS * o + STEP_HEADS * half + BANK_HEADS * b + i
                if on_vector(n, b):
                    nc.vector.tensor_scalar_add(
                        out=biased[n][:, BANK_HEADS * b + i, :],
                        in0=accs[n, b][:, i, :],
                        scalar1=bias_col[s][:, col : col + 1],
                    )
                else:
                    nc.scalar.activation(
                        out=biased[n][:, BANK_HEADS * b + i, :],
                        in_=accs[n, b][:, i, :],
                        func=ACT.Identity,
                        bias=bias_col[s][:, col : col + 1],
                        scale=1.0,
                    )

        def measure(n, j):
            if j == 0:
                sumsq[n] = work.tile([P, GROUP_TILES * STEP_HEADS], F32, name="sumsq")
                backs[n] = []
            back = psum_back.tile([P, STEP_HEADS, HEAD], F32, tag="back")
            backs[n].append(back)
            for i in range(STEP_HEADS):
                nc.tensor.transpose(back[:, i, :], biased[n][:, i, P * j : P * (j + 1)], ident[:])
            for i in range(STEP_HEADS):
                squares = work.tile([P, HEAD], F32, name="squares")
                col = STEP_HEADS * j + i
                nc.scalar.activation(
                    out=squares[:], in_=back[:, i, :], func=ACT.Square, accum_out=sumsq[n][:, col : col + 1]
                )

        def root(n):
            inv_rms[n] = work.tile([P, GROUP_TILES * STEP_HEADS], F32, name="inv_rms")
            nc.scalar.activation(
                out=inv_rms[n][:], in_=sumsq[n][:], func=ACT.Abs_reciprocal_sqrt, bias=eps[:, 0:1], scale=1.0 / HEAD
            )

        def rotate(n, between):
            g, o, half = steps[n]
            s = min(g, 1)
            r0, r1 = stream_rows[s]
            merged = n < MERGED_STEPS
            products = work.tile([P, GROUP_TILES * STEP_HEADS, 2, HEAD], F32, name="products")
            result = work.tile([P, GROUP_TILES * STEP_HEADS, PAIRS, 2], F32, name="result")
            for j in range(GROUP_TILES):
                if j == 1 and between is not None:
                    add_bias(between, 1)
                t = GROUP_TILES * g + j
                back = backs[n][j]
                last = (n, j) == (len(steps) - 1, GROUP_TILES - 1)
                on_vector_add = n == len(steps) - 1
                piece_heads = STEP_HEADS // LAST_PIECES if last else STEP_HEADS
                for i0 in range(0, STEP_HEADS, piece_heads):
                    for i in range(i0, i0 + piece_heads):
                        r = inv_rms[n][:, STEP_HEADS * j + i : STEP_HEADS * j + i + 1]
                        nc.vector.scalar_tensor_tensor(
                            out=products[:, STEP_HEADS * j + i, :, :],
                            in0=back[:, i, :].unsqueeze(1).to_broadcast([P, 2, HEAD]),
                            scalar=r,
                            in1=table[o][:, t, :, :],
                            op0=ALU.mult,
                            op1=ALU.mult,
                        )
                    if merged and j == 0:
                        continue
                    first_block = 0 if merged else STEP_HEADS * j + i0
                    blocks = slice(first_block, STEP_HEADS * j + i0 + piece_heads)
                    adder = nc.vector if on_vector_add else nc.gpsimd
                    adder.tensor_tensor(
                        out=result[:, blocks, :, :],
                        in0=products[:, blocks, 0, :].rearrange("p h (c e) -> p h c e", e=2),
                        in1=products[:, blocks, 1, :].rearrange("p h (c e) -> p h c e", e=2)[:, :, :, ::-1],
                        op=ALU.add,
                    )
                    for b0 in range(first_block, blocks.stop, piece_heads):
                        first = HEAD * (STEP_HEADS * half + b0 % STEP_HEADS)
                        tile_of_stream = GROUP_TILES * g + b0 // STEP_HEADS - stream_tiles[s][0]
                        nc.sync.dma_start(
                            out=by_tiles(outs[o][r0:r1, first : first + HEAD * piece_heads], s)[:, tile_of_stream, :],
                            in_=result[:, b0 : b0 + piece_heads, :, :].rearrange("p h c e -> p (h c e)"),
                        )

        flip_group(1, at_head=True)
        bias_columns(1)
        for j in range(GROUP_TILES):
            flip_tile(2, j, True)
        quantise_group(1)
        for j in range(GROUP_TILES):
            regroup_tile(2, j)
        quantise_group(2)
        cos_table(1, 0)
        sin_table(1, 0, nc.vector)
        cos_table(1, 1)
        sin_table(1, 1, nc.gpsimd)
        for o in range(2):
            cos_table(0, o)
        for n in range(len(steps) + 2):
            if n == TEXT_PREP_ROUND - 1:
                widen_late_bias(0)
            if n == TEXT_PREP_ROUND:
                flip_group(TEXT_GROUP)
            if n == TEXT_PREP_ROUND + 1:
                flip_late_bias(0)
            if n == LAST_IMAGE_PREP_ROUND:
                flip_group(3)
            for part in range(2):
                if n < len(steps):
                    project(n, part)
                if 1 <= n <= len(steps):
                    measure(n - 1, part)
            if 1 <= n <= len(steps):
                root(n - 1)
            if n >= 2:
                rotate(n - 2, n if n < len(steps) and on_vector(n, 1) else None)
            elif on_vector(n, 1):
                add_bias(n, 1)
            if n == 1:
                for o in range(2):
                    sin_table(0, o, nc.vector)
            if n == LAST_IMAGE_PREP_ROUND:
                quantise_group(3)
            if n == TEXT_PREP_ROUND:
                quantise_group(TEXT_GROUP)
